import numpy as np
import ml_dtypes


def mxq(x, axis, fmt="e4m3"):
    dtype, down = {"e4m3": (ml_dtypes.float8_e4m3fn, 7), "e5m2": (ml_dtypes.float8_e5m2, 14)}[fmt]
    v = np.moveaxis(np.asarray(x, np.float32).astype(ml_dtypes.bfloat16).astype(np.float64), axis, -1)
    blocks = v.reshape(v.shape[:-1] + (-1, 32))
    amax = np.abs(blocks).max(-1, keepdims=True)
    byte = np.maximum(np.where(amax > 0, np.frexp(amax)[1] - 1 + 127, 0) - down, 1)
    scale = np.exp2(byte - 127.0)
    codes = (blocks / scale).astype(np.float32).astype(dtype).astype(np.float64)
    return np.moveaxis((codes * scale).reshape(v.shape), -1, axis)


WIDE = False


def mx_kscale(k):
    if not WIDE:
        return np.ones(k)
    levels = np.array([10, -10, 5, -5, 0])
    if k % 512:
        return np.exp2(np.random.permutation(np.resize(levels, k // 32))).repeat(32)
    a = np.empty((k // 512, 16))
    for p in range(k // 512):
        a[p, :8] = np.random.permutation(np.resize(levels, 8))
        for g in range(8):
            far = levels[np.abs(levels - a[p, g]) >= 10]
            a[p, g + 8] = far[np.random.randint(len(far))]
    return np.exp2(a.ravel()).repeat(32)


BF16 = ml_dtypes.bfloat16


def bf(x):
    return np.asarray(x, np.float32).astype(BF16)


def f64(x):
    return np.asarray(x).astype(np.float64)


B, S, D_IN, MID, FFN, D_OUT, R = 8, 1024, 256, 512, 512, 256, 16
LN_EPS = 1e-5


def silu(v):
    return v / (1.0 + np.exp(-v))


def layer_norm(x, gamma, beta):
    m = np.mean(x, axis=-1, keepdims=True)
    v = np.mean(np.square(x - m), axis=-1, keepdims=True)
    return (x - m) / np.sqrt(v + LN_EPS) * gamma + beta


def setup_inputs():
    t, s = mx_kscale(FFN), mx_kscale(MID)
    return {"h": bf(silu(np.random.standard_normal((B, S, FFN))) * t),
            "w_f2": bf(np.random.standard_normal((MID, FFN)) / np.sqrt(FFN) / t),
            "b_f2": bf(0.1 * np.random.standard_normal(MID)),
            "res1": bf(0.7 * np.random.standard_normal((B, S, MID))),
            "g2": bf((1.0 + 0.1 * np.random.standard_normal(MID)) * s),
            "be2": bf(0.1 * np.random.standard_normal(MID) * s),
            "w_h": bf(np.random.standard_normal((D_OUT, MID)) / np.sqrt(MID) / s),
            "b_h": bf(0.1 * np.random.standard_normal(D_OUT))}


def reference(h, w_f2, b_f2, res1, g2, be2, w_h, b_h):
    ffn = (mxq(f64(h), 2, "e4m3") @ mxq(f64(w_f2), 1, "e4m3").T) + f64(b_f2)
    res2 = f64(res1) + ffn
    norm2 = layer_norm(res2, f64(g2), f64(be2))
    return (mxq(norm2, 2, "e4m3") @ mxq(f64(w_h), 1, "e4m3").T) + f64(b_h)

@@ -1,0 +1,301 @@
+from contextlib import ExitStack
+
+import concourse.mybir as mybir
+from concourse.masks import make_identity
+
+F32 = mybir.dt.float32
+BF16 = mybir.dt.bfloat16
+U32 = mybir.dt.uint32
+U8 = mybir.dt.uint8
+FP8X4 = mybir.dt.float8_e4m3fn_x4
+ADD = mybir.AluOpType.add
+MULT = mybir.AluOpType.mult
+ACT = mybir.ActivationFunctionType
+
+P = 128
+PACK = 4
+BANK = 512
+TOKENS = 8 * 1024
+FFN = 512
+MID = 512
+D_OUT = 256
+LN_EPS = 1e-5
+GROUP = 4
+GROUPS = TOKENS // (P * GROUP)
+GPSIMD_TILES = 3
+
+FLOPS = 2 * TOKENS * FFN * MID + 2 * TOKENS * MID * D_OUT
+
+
+def transpose_bf16_rows(nc, new_bank, work, rows, ident):
+    words = rows.bitcast(F32)
+    pair_grouped = work.tile([P, GROUP * P * PACK], BF16, align_bytes=64)
+    grouped_words = pair_grouped[:].bitcast(F32).rearrange("p (j r u) -> p j r u", j=GROUP, u=2)
+    for b in range(GROUP // 2):
+        pairs_t = new_bank()
+        for j in range(2):
+            for u in range(2):
+                first = (2 * b + j) * 2 * P
+                nc.tensor.transpose(
+                    pairs_t[:, (2 * j + u) * P : (2 * j + u + 1) * P], words[:, first + u : first + 2 * P : 2], ident
+                )
+        nc.scalar.copy(
+            out=grouped_words[:, 2 * b : 2 * b + 2],
+            in_=pairs_t[:].rearrange("p (j u r) -> p j r u", j=2, u=2),
+        )
+    return pair_grouped
+
+
+def transpose_f32_rows(nc, new_bank, work, row_tiles, ident, gain, shift):
+    width = len(row_tiles) * P
+    planes = work.tile([P, PACK, width], BF16)
+    for c in range(PACK):
+        chunk_t = new_bank()
+        for r, x in enumerate(row_tiles):
+            nc.tensor.transpose(chunk_t[:, r * P : (r + 1) * P], x[:, c:MID:PACK], ident)
+        nc.scalar.activation(
+            out=planes[:, c, :], in_=chunk_t[:, 0:width], func=ACT.Identity, scale=gain[c], bias=shift[c]
+        )
+    return planes
+
+
+def group_planes(nc, work, planes, width):
+    chunk_grouped = work.tile([P, width * PACK], BF16, align_bytes=64)
+    nc.gpsimd.tensor_scalar(
+        out=chunk_grouped[:].rearrange("p (w c) -> p w c", c=PACK),
+        in0=planes[:].rearrange("p c w -> p w c"),
+        scalar1=1.0,
+        scalar2=0.0,
+        op0=MULT,
+        op1=ADD,
+    )
+    return chunk_grouped
+
+
+def tile_tsh_mid_block_pb_t_kernel(tc, h, w_f2, b_f2, res1, g2, be2, w_h, b_h, out):
+    nc = tc.nc
+    h_rows = h.flatten_outer_dims().rearrange("(p j) k -> p (j k)", p=P)
+    res_rows = res1.flatten_outer_dims().rearrange("(p j) m -> p (j m)", p=P)
+    out_rows = out.flatten_outer_dims().rearrange("(p j) o -> p (j o)", p=P)
+
+    with ExitStack() as ctx:
+        const = ctx.enter_context(tc.tile_pool(name="const", bufs=1))
+        loads = ctx.enter_context(tc.tile_pool(name="loads", bufs=4))
+        work = ctx.enter_context(tc.tile_pool(name="work", bufs=3))
+        bias_bank = ctx.enter_context(tc.psum_pool(name="bias_bank", bufs=1))
+        ring = ctx.enter_context(tc.psum_pool(name="ring", bufs=7))
+
+        def new_bank():
+            return ring.tile([P, BANK], F32, name="bank", tag="bank")
+
+        ident = const.tile([P, P], F32)
+        make_identity(nc, ident[:])
+        eps = const.tile([P, 1], F32)
+        nc.vector.memset(eps[:], LN_EPS)
+
+        w1_sb = const.tile([P, GROUP * FFN], BF16)
+        nc.sync.dma_start(
+            out=w1_sb[:].rearrange("p (r k) -> p r k", r=GROUP), in_=w_f2.rearrange("(r p) k -> p r k", p=P)
+        )
+        w1_codes = const.tile([P, MID], U32, align_bytes=64)
+        w1_scales = const.tile([P, MID], U8, align_bytes=64)
+        w1_grouped = transpose_bf16_rows(nc, new_bank, work, w1_sb[:], ident[:])
+        nc.vector.quantize_mx(out=w1_codes[:].bitcast(FP8X4), scales=w1_scales[:], in_=w1_grouped[:])
+
+        bias_rows = const.tile([P, MID + D_OUT], BF16)
+        nc.vector.memset(bias_rows[:], 0.0)
+        nc.scalar.dma_start(out=bias_rows[0:1, 0:MID], in_=b_f2.rearrange("(o m) -> o m", o=1))
+        nc.scalar.dma_start(out=bias_rows[0:1, MID : MID + D_OUT], in_=b_h.rearrange("(o m) -> o m", o=1))
+        ones = const.tile([P, P], BF16)
+        nc.vector.memset(ones[:], 1.0)
+        b1_all = bias_bank.tile([P, MID], F32)
+        nc.tensor.matmul(out=b1_all[:], lhsT=ones[:], rhs=bias_rows[:, 0:MID], start=True, stop=True)
+        b2_all = const.tile([P, D_OUT], F32)
+        b2_spread = new_bank()
+        nc.tensor.matmul(
+            out=b2_spread[:, 0:D_OUT], lhsT=ones[:], rhs=bias_rows[:, MID : MID + D_OUT], start=True, stop=True
+        )
+        nc.vector.tensor_copy(out=b2_all[:], in_=b2_spread[:, 0:D_OUT])
+
+        vec_rows = const.tile([P, MID], BF16)
+        nc.vector.memset(vec_rows[:], 0.0)
+        nc.scalar.dma_start(out=vec_rows[0:1, :], in_=g2.rearrange("(o m) -> o m", o=1))
+        nc.scalar.dma_start(out=vec_rows[1:2, :], in_=be2.rearrange("(o m) -> o m", o=1))
+        vec_rows_f32 = const.tile([P, MID], F32)
+        nc.vector.tensor_copy(out=vec_rows_f32[:], in_=vec_rows[:])
+        vec_t = new_bank()
+        for c in range(PACK):
+            nc.tensor.transpose(vec_t[:, c * P : (c + 1) * P], vec_rows_f32[:, c:MID:PACK], ident[:])
+        vec_cols = const.tile([P, PACK, 2], F32)
+        nc.vector.tensor_copy(out=vec_cols[:], in_=vec_t[:].rearrange("p (c v) -> p c v", c=PACK)[:, :, 0:2])
+        gain = [vec_cols[:, c, 0:1] for c in range(PACK)]
+        shift = [vec_cols[:, c, 1:2] for c in range(PACK)]
+
+        w2_sb = const.tile([P, D_OUT // P, MID], BF16)
+        nc.scalar.dma_start(out=w2_sb[:], in_=w_h.rearrange("(r p) m -> p r m", p=P))
+        w2_f32 = const.tile([P, D_OUT // P, MID], F32)
+        nc.vector.tensor_copy(out=w2_f32[:], in_=w2_sb[:])
+        w2_codes = const.tile([P, D_OUT], U32, align_bytes=64)
+        w2_scales = const.tile([P, D_OUT], U8, align_bytes=64)
+        w2_planes = transpose_f32_rows(
+            nc, new_bank, work, [w2_f32[:, r, :] for r in range(D_OUT // P)], ident[:], [1.0] * PACK, [0.0] * PACK
+        )
+        w2_grouped = group_planes(nc, work, w2_planes, D_OUT)
+        nc.vector.quantize_mx(out=w2_codes[:].bitcast(FP8X4), scales=w2_scales[:], in_=w2_grouped[:])
+
+        h_in, res_in, h_grouped, h_packed = {}, {}, {}, {}
+        res_biased, res2_of, sums_of, neg_mean_of, std_of, normed_of = {}, {}, {}, {}, {}, {}
+        n_planes, n_grouped, n_packed = {}, {}, {}
+
+        def load(g):
+            h_sb = loads.tile([P, GROUP * FFN], BF16)
+            nc.sync.dma_start(out=h_sb[:], in_=h_rows[:, g * GROUP * FFN : (g + 1) * GROUP * FFN])
+            res_sb = loads.tile([P, GROUP * MID], BF16)
+            nc.sync.dma_start(out=res_sb[:], in_=res_rows[:, g * GROUP * MID : (g + 1) * GROUP * MID])
+            h_in[g], res_in[g] = h_sb, res_sb
+
+        def transpose_h(g):
+            h_grouped[g] = transpose_bf16_rows(nc, new_bank, work, h_in[g][:], ident[:])
+
+        def bias_residual(g):
+            res_b = work.tile([P, GROUP, MID], F32)
+            nc.vector.tensor_tensor(
+                out=res_b[:],
+                in0=res_in[g][:].rearrange("p (j m) -> p j m", j=GROUP),
+                in1=b1_all[:].unsqueeze(1).to_broadcast([P, GROUP, MID]),
+                op=ADD,
+            )
+            res_biased[g] = res_b
+
+        def quantise_h(g):
+            h_codes = work.tile([P, GROUP * P], U32, align_bytes=64)
+            h_scales = work.tile([P, GROUP * P], U8, align_bytes=64)
+            nc.vector.quantize_mx(out=h_codes[:].bitcast(FP8X4), scales=h_scales[:], in_=h_grouped[g][:])
+            h_packed[g] = (h_codes, h_scales)
+
+        def first_matmul(g):
+            h_codes, h_scales = h_packed[g]
+            res2 = work.tile([P, GROUP, MID], F32)
+            sums = work.tile([P, GROUP], F32)
+            for j in range(GROUP):
+                tokens = slice(j * P, (j + 1) * P)
+                ffn = new_bank()
+                nc.tensor.matmul_mx(
+                    out=ffn[:],
+                    lhsT=h_codes[:, tokens].bitcast(FP8X4),
+                    lhsT_scale=h_scales[:, tokens],
+                    rhs=w1_codes[:].bitcast(FP8X4),
+                    rhs_scale=w1_scales[:],
+                    start=True,
+                    stop=True,
+                )
+                nc.vector.scalar_tensor_tensor(
+                    out=res2[:, j, :], in0=ffn[:], scalar=1.0, in1=res_biased[g][:, j, :], op0=MULT, op1=ADD,
+                    accum_out=sums[:, j : j + 1],
+                )
+            res2_of[g], sums_of[g] = res2, sums
+
+        def negative_mean(g):
+            neg_mean = work.tile([P, GROUP], F32)
+            nc.scalar.mul(out=neg_mean[:], in_=sums_of[g][:], mul=-1.0 / MID)
+            neg_mean_of[g] = neg_mean
+
+        def deviation(g):
+            squares = work.tile([P, GROUP, MID], BF16)
+            square_sums = work.tile([P, GROUP], F32)
+            for j in range(GROUP):
+                nc.scalar.activation(
+                    out=squares[:, j, :], in_=res2_of[g][:, j, :], func=ACT.Square,
+                    bias=neg_mean_of[g][:, j : j + 1], scale=1.0, accum_out=square_sums[:, j : j + 1],
+                )
+            std = work.tile([P, GROUP], F32)
+            nc.scalar.activation(out=std[:], in_=square_sums[:], func=ACT.Sqrt, scale=1.0 / MID, bias=eps[:, 0:1])
+            std_of[g] = std
+
+        def normalise(g):
+            rstd = work.tile([P, GROUP], F32)
+            nc.vector.reciprocal(out=rstd[:], in_=std_of[g][:])
+            offset = work.tile([P, GROUP], F32)
+            nc.vector.tensor_tensor(out=offset[:], in0=neg_mean_of[g][:], in1=rstd[:], op=MULT)
+            normed = work.tile([P, GROUP, MID], F32)
+            for j in range(GPSIMD_TILES):
+                nc.gpsimd.tensor_scalar(
+                    out=normed[:, j, :], in0=res2_of[g][:, j, :], scalar1=rstd[:, j : j + 1],
+                    scalar2=offset[:, j : j + 1], op0=MULT, op1=ADD,
+                )
+            for j in range(GPSIMD_TILES, GROUP):
+                nc.scalar.activation(
+                    out=normed[:, j, :], in_=res2_of[g][:, j, :], func=ACT.Identity,
+                    scale=rstd[:, j : j + 1], bias=offset[:, j : j + 1],
+                )
+            normed_of[g] = normed
+
+        def transpose_norm(g):
+            n_planes[g] = transpose_f32_rows(
+                nc, new_bank, work, [normed_of[g][:, j, :] for j in range(GROUP)], ident[:], gain, shift
+            )
+
+        def group_norm(g):
+            n_grouped[g] = group_planes(nc, work, n_planes[g], GROUP * P)
+
+        def quantise_norm(g):
+            n_codes = work.tile([P, GROUP * P], U32, align_bytes=64)
+            n_scales = work.tile([P, GROUP * P], U8, align_bytes=64)
+            nc.vector.quantize_mx(out=n_codes[:].bitcast(FP8X4), scales=n_scales[:], in_=n_grouped[g][:])
+            n_packed[g] = (n_codes, n_scales)
+
+        def second_matmul(g):
+            n_codes, n_scales = n_packed[g]
+            result = work.tile([P, GROUP, D_OUT], F32)
+            for b in range(GROUP // 2):
+                head = new_bank()
+                for j in range(2):
+                    tokens = slice((2 * b + j) * P, (2 * b + j + 1) * P)
+                    nc.tensor.matmul_mx(
+                        out=head[:, j * D_OUT : (j + 1) * D_OUT],
+                        lhsT=n_codes[:, tokens].bitcast(FP8X4),
+                        lhsT_scale=n_scales[:, tokens],
+                        rhs=w2_codes[:].bitcast(FP8X4),
+                        rhs_scale=w2_scales[:],
+                        start=True,
+                        stop=True,
+                    )
+                nc.vector.tensor_tensor(
+                    out=result[:, 2 * b : 2 * b + 2, :],
+                    in0=head[:].rearrange("p (j o) -> p j o", j=2),
+                    in1=b2_all[:].unsqueeze(1).to_broadcast([P, 2, D_OUT]),
+                    op=ADD,
+                )
+            nc.sync.dma_start(
+                out=out_rows[:, g * GROUP * D_OUT : (g + 1) * GROUP * D_OUT],
+                in_=result[:].rearrange("p j o -> p (j o)"),
+            )
+
+        def live(g):
+            return 0 <= g < GROUPS
+
+        with tc.manual_schedule():
+            for k in range(GROUPS + 7):
+                if live(k - 5):
+                    negative_mean(k - 5)
+                    deviation(k - 5)
+                if live(k - 2):
+                    transpose_h(k - 2)
+                if live(k - 6):
+                    transpose_norm(k - 6)
+                if live(k - 4):
+                    bias_residual(k - 4)
+                if live(k - 3):
+                    quantise_h(k - 3)
+                if live(k - 7):
+                    quantise_norm(k - 7)
+                if live(k):
+                    load(k)
+                if live(k - 5):
+                    normalise(k - 5)
+                if live(k - 4):
+                    first_matmul(k - 4)
+                if live(k - 6):
+                    group_norm(k - 6)
+                if live(k - 7):
+                    second_matmul(k - 7)

@@ -20,67 +20,42 @@ FFN = 512
 MID = 512
 D_OUT = 256
 LN_EPS = 1e-5
-GROUP = 4
-GROUPS = TOKENS // (P * GROUP)
-GPSIMD_TILES = 3
+TILES = TOKENS // P
+SIZES = [1, 1] + [2] * (TILES // 2 - 2) + [1, 1]
+STARTS = [sum(SIZES[:g]) for g in range(len(SIZES))]
+GROUPS = len(SIZES)
 
 FLOPS = 2 * TOKENS * FFN * MID + 2 * TOKENS * MID * D_OUT
 
 
-def transpose_bf16_rows(nc, new_bank, work, rows, ident):
-    words = rows.bitcast(F32)
-    pair_grouped = work.tile([P, GROUP * P * PACK], BF16, align_bytes=64)
-    grouped_words = pair_grouped[:].bitcast(F32).rearrange("p (j r u) -> p j r u", j=GROUP, u=2)
-    for b in range(GROUP // 2):
+def transpose_bf16_rows(nc, new_bank, grouped, rows, ident, copies):
+    n = rows.shape[1]
+    words = rows.rearrange("p n k -> p (n k)").bitcast(F32)
+    grouped_words = grouped.bitcast(F32).rearrange("p (n r u) -> p n r u", n=n, u=2)
+    for b, first in enumerate(range(0, n, 2)):
+        count = min(2, n - first)
         pairs_t = new_bank()
-        for j in range(2):
+        for j in range(count):
+            word = (first + j) * 2 * P
             for u in range(2):
-                first = (2 * b + j) * 2 * P
                 nc.tensor.transpose(
-                    pairs_t[:, (2 * j + u) * P : (2 * j + u + 1) * P], words[:, first + u : first + 2 * P : 2], ident
+                    pairs_t[:, (2 * j + u) * P : (2 * j + u + 1) * P], words[:, word + u : word + 2 * P : 2], ident
                 )
-        nc.scalar.copy(
-            out=grouped_words[:, 2 * b : 2 * b + 2],
-            in_=pairs_t[:].rearrange("p (j u r) -> p j r u", j=2, u=2),
+        copies[b % len(copies)](
+            out=grouped_words[:, first : first + count],
+            in_=pairs_t[:, 0 : count * 2 * P].rearrange("p (j u r) -> p j r u", j=count, u=2),
         )
-    return pair_grouped
-
-
-def transpose_f32_rows(nc, new_bank, work, row_tiles, ident, gain, shift):
-    width = len(row_tiles) * P
-    planes = work.tile([P, PACK, width], BF16)
-    for c in range(PACK):
-        chunk_t = new_bank()
-        for r, x in enumerate(row_tiles):
-            nc.tensor.transpose(chunk_t[:, r * P : (r + 1) * P], x[:, c:MID:PACK], ident)
-        nc.scalar.activation(
-            out=planes[:, c, :], in_=chunk_t[:, 0:width], func=ACT.Identity, scale=gain[c], bias=shift[c]
-        )
-    return planes
-
-
-def group_planes(nc, work, planes, width):
-    chunk_grouped = work.tile([P, width * PACK], BF16, align_bytes=64)
-    nc.gpsimd.tensor_scalar(
-        out=chunk_grouped[:].rearrange("p (w c) -> p w c", c=PACK),
-        in0=planes[:].rearrange("p c w -> p w c"),
-        scalar1=1.0,
-        scalar2=0.0,
-        op0=MULT,
-        op1=ADD,
-    )
-    return chunk_grouped
 
 
 def tile_tsh_mid_block_pb_t_kernel(tc, h, w_f2, b_f2, res1, g2, be2, w_h, b_h, out):
     nc = tc.nc
-    h_rows = h.flatten_outer_dims().rearrange("(p j) k -> p (j k)", p=P)
-    res_rows = res1.flatten_outer_dims().rearrange("(p j) m -> p (j m)", p=P)
-    out_rows = out.flatten_outer_dims().rearrange("(p j) o -> p (j o)", p=P)
+    h_rows = h.flatten_outer_dims().rearrange("(p j) k -> p j k", p=P)
+    res_rows = res1.flatten_outer_dims().rearrange("(p j) m -> p j m", p=P)
+    out_rows = out.flatten_outer_dims().rearrange("(p j) o -> p j o", p=P)
 
     with ExitStack() as ctx:
         const = ctx.enter_context(tc.tile_pool(name="const", bufs=1))
-        loads = ctx.enter_context(tc.tile_pool(name="loads", bufs=4))
+        loads = ctx.enter_context(tc.tile_pool(name="loads", bufs=5))
         work = ctx.enter_context(tc.tile_pool(name="work", bufs=3))
         bias_bank = ctx.enter_context(tc.psum_pool(name="bias_bank", bufs=1))
         ring = ctx.enter_context(tc.psum_pool(name="ring", bufs=7))
@@ -93,13 +68,12 @@ def tile_tsh_mid_block_pb_t_kernel(tc, h, w_f2, b_f2, res1, g2, be2, w_h, b_h, o
         eps = const.tile([P, 1], F32)
         nc.vector.memset(eps[:], LN_EPS)
 
-        w1_sb = const.tile([P, GROUP * FFN], BF16)
-        nc.sync.dma_start(
-            out=w1_sb[:].rearrange("p (r k) -> p r k", r=GROUP), in_=w_f2.rearrange("(r p) k -> p r k", p=P)
-        )
+        w1_sb = const.tile([P, PACK, FFN], BF16)
+        nc.sync.dma_start(out=w1_sb[:], in_=w_f2.rearrange("(m t) k -> m t k", t=PACK))
+        w1_grouped = const.tile([P, PACK * FFN], BF16, align_bytes=64)
         w1_codes = const.tile([P, MID], U32, align_bytes=64)
         w1_scales = const.tile([P, MID], U8, align_bytes=64)
-        w1_grouped = transpose_bf16_rows(nc, new_bank, work, w1_sb[:], ident[:])
+        transpose_bf16_rows(nc, new_bank, w1_grouped[:], w1_sb[:], ident[:], [nc.scalar.copy, nc.vector.tensor_copy])
         nc.vector.quantize_mx(out=w1_codes[:].bitcast(FP8X4), scales=w1_scales[:], in_=w1_grouped[:])
 
         bias_rows = const.tile([P, MID + D_OUT], BF16)
@@ -109,7 +83,10 @@ def tile_tsh_mid_block_pb_t_kernel(tc, h, w_f2, b_f2, res1, g2, be2, w_h, b_h, o
         ones = const.tile([P, P], BF16)
         nc.vector.memset(ones[:], 1.0)
         b1_all = bias_bank.tile([P, MID], F32)
-        nc.tensor.matmul(out=b1_all[:], lhsT=ones[:], rhs=bias_rows[:, 0:MID], start=True, stop=True)
+        for t in range(PACK):
+            nc.tensor.matmul(
+                out=b1_all[:, t * P : (t + 1) * P], lhsT=ones[:], rhs=bias_rows[:, t:MID:PACK], start=True, stop=True
+            )
         b2_all = const.tile([P, D_OUT], F32)
         b2_spread = new_bank()
         nc.tensor.matmul(
@@ -124,60 +101,61 @@ def tile_tsh_mid_block_pb_t_kernel(tc, h, w_f2, b_f2, res1, g2, be2, w_h, b_h, o
         vec_rows_f32 = const.tile([P, MID], F32)
         nc.vector.tensor_copy(out=vec_rows_f32[:], in_=vec_rows[:])
         vec_t = new_bank()
-        for c in range(PACK):
-            nc.tensor.transpose(vec_t[:, c * P : (c + 1) * P], vec_rows_f32[:, c:MID:PACK], ident[:])
+        for t in range(PACK):
+            nc.tensor.transpose(vec_t[:, t * P : (t + 1) * P], vec_rows_f32[:, t:MID:PACK], ident[:])
         vec_cols = const.tile([P, PACK, 2], F32)
-        nc.vector.tensor_copy(out=vec_cols[:], in_=vec_t[:].rearrange("p (c v) -> p c v", c=PACK)[:, :, 0:2])
-        gain = [vec_cols[:, c, 0:1] for c in range(PACK)]
-        shift = [vec_cols[:, c, 1:2] for c in range(PACK)]
+        nc.vector.tensor_copy(out=vec_cols[:], in_=vec_t[:].rearrange("p (t v) -> p t v", t=PACK)[:, :, 0:2])
+        gain = [vec_cols[:, t, 0:1] for t in range(PACK)]
+        shift = [vec_cols[:, t, 1:2] for t in range(PACK)]
 
         w2_sb = const.tile([P, D_OUT // P, MID], BF16)
         nc.scalar.dma_start(out=w2_sb[:], in_=w_h.rearrange("(r p) m -> p r m", p=P))
-        w2_f32 = const.tile([P, D_OUT // P, MID], F32)
-        nc.vector.tensor_copy(out=w2_f32[:], in_=w2_sb[:])
+        w2_grouped = const.tile([P, D_OUT // P * MID], BF16, align_bytes=64)
         w2_codes = const.tile([P, D_OUT], U32, align_bytes=64)
         w2_scales = const.tile([P, D_OUT], U8, align_bytes=64)
-        w2_planes = transpose_f32_rows(
-            nc, new_bank, work, [w2_f32[:, r, :] for r in range(D_OUT // P)], ident[:], [1.0] * PACK, [0.0] * PACK
-        )
-        w2_grouped = group_planes(nc, work, w2_planes, D_OUT)
+        transpose_bf16_rows(nc, new_bank, w2_grouped[:], w2_sb[:], ident[:], [nc.scalar.copy])
         nc.vector.quantize_mx(out=w2_codes[:].bitcast(FP8X4), scales=w2_scales[:], in_=w2_grouped[:])
 
         h_in, res_in, h_grouped, h_packed = {}, {}, {}, {}
-        res_biased, res2_of, sums_of, neg_mean_of, std_of, normed_of = {}, {}, {}, {}, {}, {}
+        res_biased, res2_of, sums_of, neg_mean_of, rstd_of, normed_of = {}, {}, {}, {}, {}, {}
         n_planes, n_grouped, n_packed = {}, {}, {}
 
         def load(g):
-            h_sb = loads.tile([P, GROUP * FFN], BF16)
-            nc.sync.dma_start(out=h_sb[:], in_=h_rows[:, g * GROUP * FFN : (g + 1) * GROUP * FFN])
-            res_sb = loads.tile([P, GROUP * MID], BF16)
-            nc.sync.dma_start(out=res_sb[:], in_=res_rows[:, g * GROUP * MID : (g + 1) * GROUP * MID])
+            n, first = SIZES[g], STARTS[g]
+            h_sb = loads.tile([P, n, FFN], BF16)
+            nc.sync.dma_start(out=h_sb[:], in_=h_rows[:, first : first + n, :])
+            res_sb = loads.tile([P, n, MID], BF16)
+            nc.sync.dma_start(out=res_sb[:], in_=res_rows[:, first : first + n, :])
             h_in[g], res_in[g] = h_sb, res_sb
 
         def transpose_h(g):
-            h_grouped[g] = transpose_bf16_rows(nc, new_bank, work, h_in[g][:], ident[:])
+            grouped = work.tile([P, SIZES[g] * FFN], BF16, align_bytes=64)
+            transpose_bf16_rows(nc, new_bank, grouped[:], h_in[g][:], ident[:], [nc.scalar.copy])
+            h_grouped[g] = grouped
 
         def bias_residual(g):
-            res_b = work.tile([P, GROUP, MID], F32)
+            n = SIZES[g]
+            res_b = work.tile([P, n, MID], F32)
             nc.vector.tensor_tensor(
-                out=res_b[:],
-                in0=res_in[g][:].rearrange("p (j m) -> p j m", j=GROUP),
-                in1=b1_all[:].unsqueeze(1).to_broadcast([P, GROUP, MID]),
+                out=res_b[:].rearrange("p j (t m) -> p j t m", t=PACK),
+                in0=res_in[g][:].rearrange("p j (m t) -> p j t m", t=PACK),
+                in1=b1_all[:].rearrange("p (t m) -> p t m", t=PACK).unsqueeze(1).to_broadcast([P, n, PACK, P]),
                 op=ADD,
             )
             res_biased[g] = res_b
 
         def quantise_h(g):
-            h_codes = work.tile([P, GROUP * P], U32, align_bytes=64)
-            h_scales = work.tile([P, GROUP * P], U8, align_bytes=64)
+            h_codes = work.tile([P, SIZES[g] * P], U32, align_bytes=64)
+            h_scales = work.tile([P, SIZES[g] * P], U8, align_bytes=64)
             nc.vector.quantize_mx(out=h_codes[:].bitcast(FP8X4), scales=h_scales[:], in_=h_grouped[g][:])
             h_packed[g] = (h_codes, h_scales)
 
         def first_matmul(g):
+            n = SIZES[g]
             h_codes, h_scales = h_packed[g]
-            res2 = work.tile([P, GROUP, MID], F32)
-            sums = work.tile([P, GROUP], F32)
-            for j in range(GROUP):
+            res2 = work.tile([P, n, MID], F32)
+            sums = work.tile([P, n], F32)
+            for j in range(n):
                 tokens = slice(j * P, (j + 1) * P)
                 ffn = new_bank()
                 nc.tensor.matmul_mx(
@@ -195,81 +173,90 @@ def tile_tsh_mid_block_pb_t_kernel(tc, h, w_f2, b_f2, res1, g2, be2, w_h, b_h, o
                 )
             res2_of[g], sums_of[g] = res2, sums
 
-        def negative_mean(g):
-            neg_mean = work.tile([P, GROUP], F32)
+        def statistics(g):
+            n = SIZES[g]
+            neg_mean = work.tile([P, n], F32)
             nc.scalar.mul(out=neg_mean[:], in_=sums_of[g][:], mul=-1.0 / MID)
-            neg_mean_of[g] = neg_mean
-
-        def deviation(g):
-            squares = work.tile([P, GROUP, MID], BF16)
-            square_sums = work.tile([P, GROUP], F32)
-            for j in range(GROUP):
+            squares = work.tile([P, n, MID], BF16)
+            square_sums = work.tile([P, n], F32)
+            for j in range(n):
                 nc.scalar.activation(
                     out=squares[:, j, :], in_=res2_of[g][:, j, :], func=ACT.Square,
-                    bias=neg_mean_of[g][:, j : j + 1], scale=1.0, accum_out=square_sums[:, j : j + 1],
+                    bias=neg_mean[:, j : j + 1], scale=1.0, accum_out=square_sums[:, j : j + 1],
                 )
-            std = work.tile([P, GROUP], F32)
-            nc.scalar.activation(out=std[:], in_=square_sums[:], func=ACT.Sqrt, scale=1.0 / MID, bias=eps[:, 0:1])
-            std_of[g] = std
+            rstd = work.tile([P, n], F32)
+            nc.scalar.activation(
+                out=rstd[:], in_=square_sums[:], func=ACT.Abs_reciprocal_sqrt, scale=1.0 / MID, bias=eps[:, 0:1]
+            )
+            neg_mean_of[g], rstd_of[g] = neg_mean, rstd
 
         def normalise(g):
-            rstd = work.tile([P, GROUP], F32)
-            nc.vector.reciprocal(out=rstd[:], in_=std_of[g][:])
-            offset = work.tile([P, GROUP], F32)
-            nc.vector.tensor_tensor(out=offset[:], in0=neg_mean_of[g][:], in1=rstd[:], op=MULT)
-            normed = work.tile([P, GROUP, MID], F32)
-            for j in range(GPSIMD_TILES):
+            n = SIZES[g]
+            normed = work.tile([P, n, MID], F32)
+            for j in range(n):
                 nc.gpsimd.tensor_scalar(
-                    out=normed[:, j, :], in0=res2_of[g][:, j, :], scalar1=rstd[:, j : j + 1],
-                    scalar2=offset[:, j : j + 1], op0=MULT, op1=ADD,
-                )
-            for j in range(GPSIMD_TILES, GROUP):
-                nc.scalar.activation(
-                    out=normed[:, j, :], in_=res2_of[g][:, j, :], func=ACT.Identity,
-                    scale=rstd[:, j : j + 1], bias=offset[:, j : j + 1],
+                    out=normed[:, j, :], in0=res2_of[g][:, j, :], scalar1=neg_mean_of[g][:, j : j + 1],
+                    scalar2=rstd_of[g][:, j : j + 1], op0=ADD, op1=MULT,
                 )
             normed_of[g] = normed
 
         def transpose_norm(g):
-            n_planes[g] = transpose_f32_rows(
-                nc, new_bank, work, [normed_of[g][:, j, :] for j in range(GROUP)], ident[:], gain, shift
-            )
+            n = SIZES[g]
+            planes = work.tile([P, PACK, n * P], BF16)
+            for half in range(2):
+                chunks = new_bank()
+                for e in range(2):
+                    t = 2 * half + e
+                    for j in range(n):
+                        nc.tensor.transpose(
+                            chunks[:, (e * n + j) * P : (e * n + j + 1) * P], normed_of[g][:, j, t * P : (t + 1) * P], ident[:]
+                        )
+                for e in range(2):
+                    t = 2 * half + e
+                    nc.scalar.activation(
+                        out=planes[:, t, :], in_=chunks[:, e * n * P : (e + 1) * n * P], func=ACT.Identity,
+                        scale=gain[t], bias=shift[t],
+                    )
+            n_planes[g] = planes
 
         def group_norm(g):
-            n_grouped[g] = group_planes(nc, work, n_planes[g], GROUP * P)
+            grouped = work.tile([P, SIZES[g] * P * PACK], BF16, align_bytes=64)
+            nc.gpsimd.tensor_scalar(
+                out=grouped[:].rearrange("p (w t) -> p w t", t=PACK),
+                in0=n_planes[g][:].rearrange("p t w -> p w t"),
+                scalar1=1.0, scalar2=0.0, op0=MULT, op1=ADD,
+            )
+            n_grouped[g] = grouped
 
         def quantise_norm(g):
-            n_codes = work.tile([P, GROUP * P], U32, align_bytes=64)
-            n_scales = work.tile([P, GROUP * P], U8, align_bytes=64)
+            n_codes = work.tile([P, SIZES[g] * P], U32, align_bytes=64)
+            n_scales = work.tile([P, SIZES[g] * P], U8, align_bytes=64)
             nc.vector.quantize_mx(out=n_codes[:].bitcast(FP8X4), scales=n_scales[:], in_=n_grouped[g][:])
             n_packed[g] = (n_codes, n_scales)
 
         def second_matmul(g):
+            n, first = SIZES[g], STARTS[g]
             n_codes, n_scales = n_packed[g]
-            result = work.tile([P, GROUP, D_OUT], F32)
-            for b in range(GROUP // 2):
-                head = new_bank()
-                for j in range(2):
-                    tokens = slice((2 * b + j) * P, (2 * b + j + 1) * P)
-                    nc.tensor.matmul_mx(
-                        out=head[:, j * D_OUT : (j + 1) * D_OUT],
-                        lhsT=n_codes[:, tokens].bitcast(FP8X4),
-                        lhsT_scale=n_scales[:, tokens],
-                        rhs=w2_codes[:].bitcast(FP8X4),
-                        rhs_scale=w2_scales[:],
-                        start=True,
-                        stop=True,
-                    )
-                nc.vector.tensor_tensor(
-                    out=result[:, 2 * b : 2 * b + 2, :],
-                    in0=head[:].rearrange("p (j o) -> p j o", j=2),
-                    in1=b2_all[:].unsqueeze(1).to_broadcast([P, 2, D_OUT]),
-                    op=ADD,
+            result = work.tile([P, n, D_OUT], F32)
+            head = new_bank()
+            for j in range(n):
+                tokens = slice(j * P, (j + 1) * P)
+                nc.tensor.matmul_mx(
+                    out=head[:, j * D_OUT : (j + 1) * D_OUT],
+                    lhsT=n_codes[:, tokens].bitcast(FP8X4),
+                    lhsT_scale=n_scales[:, tokens],
+                    rhs=w2_codes[:].bitcast(FP8X4),
+                    rhs_scale=w2_scales[:],
+                    start=True,
+                    stop=True,
                 )
-            nc.sync.dma_start(
-                out=out_rows[:, g * GROUP * D_OUT : (g + 1) * GROUP * D_OUT],
-                in_=result[:].rearrange("p j o -> p (j o)"),
+            nc.vector.tensor_tensor(
+                out=result[:],
+                in0=head[:, 0 : n * D_OUT].rearrange("p (j o) -> p j o", j=n),
+                in1=b2_all[:].unsqueeze(1).to_broadcast([P, n, D_OUT]),
+                op=ADD,
             )
+            nc.sync.dma_start(out=out_rows[:, first : first + n, :], in_=result[:])
 
         def live(g):
             return 0 <= g < GROUPS
@@ -277,8 +264,7 @@ def tile_tsh_mid_block_pb_t_kernel(tc, h, w_f2, b_f2, res1, g2, be2, w_h, b_h, o
         with tc.manual_schedule():
             for k in range(GROUPS + 7):
                 if live(k - 5):
-                    negative_mean(k - 5)
-                    deviation(k - 5)
+                    statistics(k - 5)
                 if live(k - 2):
                     transpose_h(k - 2)
                 if live(k - 6):

@@ -57,6 +57,7 @@ def tile_tsh_mid_block_pb_t_kernel(tc, h, w_f2, b_f2, res1, g2, be2, w_h, b_h, o
         const = ctx.enter_context(tc.tile_pool(name="const", bufs=1))
         loads = ctx.enter_context(tc.tile_pool(name="loads", bufs=5))
         work = ctx.enter_context(tc.tile_pool(name="work", bufs=3))
+        ahead = ctx.enter_context(tc.tile_pool(name="ahead", bufs=5))
         bias_bank = ctx.enter_context(tc.psum_pool(name="bias_bank", bufs=1))
         ring = ctx.enter_context(tc.psum_pool(name="ring", bufs=7))
 
@@ -67,54 +68,67 @@ def tile_tsh_mid_block_pb_t_kernel(tc, h, w_f2, b_f2, res1, g2, be2, w_h, b_h, o
         make_identity(nc, ident[:])
         eps = const.tile([P, 1], F32)
         nc.vector.memset(eps[:], LN_EPS)
+        bias_rows = const.tile([P, MID + D_OUT], BF16)
+        nc.vector.memset(bias_rows[:], 0.0)
+        ones = const.tile([P, P], BF16)
+        nc.vector.memset(ones[:], 1.0)
+        vec_rows = const.tile([P, MID], BF16)
+        nc.vector.memset(vec_rows[:], 0.0)
+        table_warm = const.tile([P, 1], F32)
+        nc.scalar.activation(out=table_warm[:], in_=eps[:], func=ACT.Abs_reciprocal_sqrt)
 
         w1_sb = const.tile([P, PACK, FFN], BF16)
-        nc.sync.dma_start(out=w1_sb[:], in_=w_f2.rearrange("(m t) k -> m t k", t=PACK))
         w1_grouped = const.tile([P, PACK * FFN], BF16, align_bytes=64)
         w1_codes = const.tile([P, MID], U32, align_bytes=64)
         w1_scales = const.tile([P, MID], U8, align_bytes=64)
-        transpose_bf16_rows(nc, new_bank, w1_grouped[:], w1_sb[:], ident[:], [nc.scalar.copy, nc.vector.tensor_copy])
-        nc.vector.quantize_mx(out=w1_codes[:].bitcast(FP8X4), scales=w1_scales[:], in_=w1_grouped[:])
-
-        bias_rows = const.tile([P, MID + D_OUT], BF16)
-        nc.vector.memset(bias_rows[:], 0.0)
-        nc.scalar.dma_start(out=bias_rows[0:1, 0:MID], in_=b_f2.rearrange("(o m) -> o m", o=1))
-        nc.scalar.dma_start(out=bias_rows[0:1, MID : MID + D_OUT], in_=b_h.rearrange("(o m) -> o m", o=1))
-        ones = const.tile([P, P], BF16)
-        nc.vector.memset(ones[:], 1.0)
         b1_all = bias_bank.tile([P, MID], F32)
-        for t in range(PACK):
-            nc.tensor.matmul(
-                out=b1_all[:, t * P : (t + 1) * P], lhsT=ones[:], rhs=bias_rows[:, t:MID:PACK], start=True, stop=True
-            )
         b2_all = const.tile([P, D_OUT], F32)
-        b2_spread = new_bank()
-        nc.tensor.matmul(
-            out=b2_spread[:, 0:D_OUT], lhsT=ones[:], rhs=bias_rows[:, MID : MID + D_OUT], start=True, stop=True
-        )
-        nc.vector.tensor_copy(out=b2_all[:], in_=b2_spread[:, 0:D_OUT])
-
-        vec_rows = const.tile([P, MID], BF16)
-        nc.vector.memset(vec_rows[:], 0.0)
-        nc.scalar.dma_start(out=vec_rows[0:1, :], in_=g2.rearrange("(o m) -> o m", o=1))
-        nc.scalar.dma_start(out=vec_rows[1:2, :], in_=be2.rearrange("(o m) -> o m", o=1))
         vec_rows_f32 = const.tile([P, MID], F32)
-        nc.vector.tensor_copy(out=vec_rows_f32[:], in_=vec_rows[:])
-        vec_t = new_bank()
-        for t in range(PACK):
-            nc.tensor.transpose(vec_t[:, t * P : (t + 1) * P], vec_rows_f32[:, t:MID:PACK], ident[:])
         vec_cols = const.tile([P, PACK, 2], F32)
-        nc.vector.tensor_copy(out=vec_cols[:], in_=vec_t[:].rearrange("p (t v) -> p t v", t=PACK)[:, :, 0:2])
         gain = [vec_cols[:, t, 0:1] for t in range(PACK)]
         shift = [vec_cols[:, t, 1:2] for t in range(PACK)]
-
         w2_sb = const.tile([P, D_OUT // P, MID], BF16)
-        nc.scalar.dma_start(out=w2_sb[:], in_=w_h.rearrange("(r p) m -> p r m", p=P))
         w2_grouped = const.tile([P, D_OUT // P * MID], BF16, align_bytes=64)
         w2_codes = const.tile([P, D_OUT], U32, align_bytes=64)
         w2_scales = const.tile([P, D_OUT], U8, align_bytes=64)
-        transpose_bf16_rows(nc, new_bank, w2_grouped[:], w2_sb[:], ident[:], [nc.scalar.copy])
-        nc.vector.quantize_mx(out=w2_codes[:].bitcast(FP8X4), scales=w2_scales[:], in_=w2_grouped[:])
+
+        def load_first_weights():
+            w_rows = w_f2.rearrange("(m t) k -> m t k", t=PACK)
+            for half in (slice(0, 2), slice(2, 4)):
+                nc.sync.dma_start(out=w1_sb[:, half, :], in_=w_rows[:, half, :])
+            nc.scalar.dma_start(out=bias_rows[0:1, 0:MID], in_=b_f2.rearrange("(o m) -> o m", o=1))
+            nc.scalar.dma_start(out=bias_rows[0:1, MID : MID + D_OUT], in_=b_h.rearrange("(o m) -> o m", o=1))
+
+        def load_last_weights():
+            nc.sync.dma_start(out=vec_rows[0:1, :], in_=g2.rearrange("(o m) -> o m", o=1))
+            nc.sync.dma_start(out=vec_rows[1:2, :], in_=be2.rearrange("(o m) -> o m", o=1))
+            nc.sync.dma_start(out=w2_sb[:], in_=w_h.rearrange("(r p) m -> p r m", p=P))
+
+        def prepare_first_weights():
+            for t in range(PACK):
+                nc.tensor.matmul(
+                    out=b1_all[:, t * P : (t + 1) * P], lhsT=ones[:], rhs=bias_rows[:, t:MID:PACK], start=True, stop=True
+                )
+            transpose_bf16_rows(nc, new_bank, w1_grouped[:], w1_sb[:], ident[:], [nc.scalar.copy, nc.vector.tensor_copy])
+            nc.vector.quantize_mx(out=w1_codes[:].bitcast(FP8X4), scales=w1_scales[:], in_=w1_grouped[:])
+
+        def prepare_last_weights():
+            b2_spread = new_bank()
+            nc.tensor.matmul(
+                out=b2_spread[:, 0:D_OUT], lhsT=ones[:], rhs=bias_rows[:, MID : MID + D_OUT], start=True, stop=True
+            )
+            nc.scalar.copy(out=b2_all[:], in_=b2_spread[:, 0:D_OUT])
+            nc.gpsimd.tensor_scalar(
+                out=vec_rows_f32[:], in0=vec_rows[:], scalar1=1.0, scalar2=0.0, op0=MULT, op1=ADD
+            )
+            vec_t = new_bank()
+            for t in range(PACK):
+                nc.tensor.transpose(vec_t[:, t * P : (t + 1) * P], vec_rows_f32[:, t:MID:PACK], ident[:])
+            nc.scalar.copy(out=vec_cols[:], in_=vec_t[:].rearrange("p (t v) -> p t v", t=PACK)[:, :, 0:2])
+            transpose_bf16_rows(nc, new_bank, w2_grouped[:], w2_sb[:], ident[:], [nc.scalar.copy])
+
+        def quantise_last_weight():
+            nc.vector.quantize_mx(out=w2_codes[:].bitcast(FP8X4), scales=w2_scales[:], in_=w2_grouped[:])
 
         h_in, res_in, h_grouped, h_packed = {}, {}, {}, {}
         res_biased, res2_of, sums_of, neg_mean_of, rstd_of, normed_of = {}, {}, {}, {}, {}, {}
@@ -135,7 +149,7 @@ def tile_tsh_mid_block_pb_t_kernel(tc, h, w_f2, b_f2, res1, g2, be2, w_h, b_h, o
 
         def bias_residual(g):
             n = SIZES[g]
-            res_b = work.tile([P, n, MID], F32)
+            res_b = ahead.tile([P, n, MID], F32)
             nc.vector.tensor_tensor(
                 out=res_b[:].rearrange("p j (t m) -> p j t m", t=PACK),
                 in0=res_in[g][:].rearrange("p j (m t) -> p j t m", t=PACK),
@@ -190,14 +204,24 @@ def tile_tsh_mid_block_pb_t_kernel(tc, h, w_f2, b_f2, res1, g2, be2, w_h, b_h, o
             )
             neg_mean_of[g], rstd_of[g] = neg_mean, rstd
 
+        def on_scalar(g, j):
+            return g % 2 == 1 and j == 1
+
         def normalise(g):
             n = SIZES[g]
             normed = work.tile([P, n, MID], F32)
             for j in range(n):
-                nc.gpsimd.tensor_scalar(
-                    out=normed[:, j, :], in0=res2_of[g][:, j, :], scalar1=neg_mean_of[g][:, j : j + 1],
-                    scalar2=rstd_of[g][:, j : j + 1], op0=ADD, op1=MULT,
-                )
+                neg_mean, rstd = neg_mean_of[g][:, j : j + 1], rstd_of[g][:, j : j + 1]
+                if on_scalar(g, j):
+                    offset = work.tile([P, 1], F32)
+                    nc.scalar.activation(out=offset[:], in_=neg_mean, func=ACT.Identity, scale=rstd)
+                    nc.scalar.activation(
+                        out=normed[:, j, :], in_=res2_of[g][:, j, :], func=ACT.Identity, scale=rstd, bias=offset[:]
+                    )
+                else:
+                    nc.gpsimd.tensor_scalar(
+                        out=normed[:, j, :], in0=res2_of[g][:, j, :], scalar1=neg_mean, scalar2=rstd, op0=ADD, op1=MULT
+                    )
             normed_of[g] = normed
 
         def transpose_norm(g):
@@ -262,25 +286,34 @@ def tile_tsh_mid_block_pb_t_kernel(tc, h, w_f2, b_f2, res1, g2, be2, w_h, b_h, o
             return 0 <= g < GROUPS
 
         with tc.manual_schedule():
+            load_first_weights()
             for k in range(GROUPS + 7):
                 if live(k - 5):
                     statistics(k - 5)
+                if k == 2:
+                    prepare_first_weights()
                 if live(k - 2):
                     transpose_h(k - 2)
+                if k == 3:
+                    prepare_last_weights()
+                if live(k - 5):
+                    normalise(k - 5)
                 if live(k - 6):
                     transpose_norm(k - 6)
-                if live(k - 4):
-                    bias_residual(k - 4)
+                if live(k - 2):
+                    bias_residual(k - 2)
                 if live(k - 3):
                     quantise_h(k - 3)
                 if live(k - 7):
                     quantise_norm(k - 7)
                 if live(k):
                     load(k)
-                if live(k - 5):
-                    normalise(k - 5)
+                if k == 1:
+                    load_last_weights()
                 if live(k - 4):
                     first_matmul(k - 4)
+                if k == 5:
+                    quantise_last_weight()
                 if live(k - 6):
                     group_norm(k - 6)
                 if live(k - 7):

@@ -21,28 +21,37 @@ MID = 512
 D_OUT = 256
 LN_EPS = 1e-5
 TILES = TOKENS // P
-SIZES = [1, 1] + [2] * (TILES // 2 - 2) + [1, 1]
+SIZES = [1, 1, 2] + [4] * (TILES // 4 - 2) + [2, 1, 1]
+VECTOR_GROUPS = 3
 STARTS = [sum(SIZES[:g]) for g in range(len(SIZES))]
 GROUPS = len(SIZES)
 
 FLOPS = 2 * TOKENS * FFN * MID + 2 * TOKENS * MID * D_OUT
 
 
-def transpose_bf16_rows(nc, new_bank, grouped, rows, ident, copies):
+def transpose_words(nc, new_bank, rows, ident):
     n = rows.shape[1]
     words = rows.rearrange("p n k -> p (n k)").bitcast(F32)
-    grouped_words = grouped.bitcast(F32).rearrange("p (n r u) -> p n r u", n=n, u=2)
-    for b, first in enumerate(range(0, n, 2)):
-        count = min(2, n - first)
+    banks = []
+    for first in range(0, n, 2):
         pairs_t = new_bank()
-        for j in range(count):
+        for j in range(min(2, n - first)):
             word = (first + j) * 2 * P
             for u in range(2):
                 nc.tensor.transpose(
                     pairs_t[:, (2 * j + u) * P : (2 * j + u + 1) * P], words[:, word + u : word + 2 * P : 2], ident
                 )
+        banks.append(pairs_t)
+    return banks
+
+
+def group_words(banks, grouped, copies):
+    n = grouped.shape[1] // FFN
+    grouped_words = grouped.bitcast(F32).rearrange("p (n r u) -> p n r u", n=n, u=2)
+    for b, pairs_t in enumerate(banks):
+        count = min(2, n - 2 * b)
         copies[b % len(copies)](
-            out=grouped_words[:, first : first + count],
+            out=grouped_words[:, 2 * b : 2 * b + count],
             in_=pairs_t[:, 0 : count * 2 * P].rearrange("p (j u r) -> p j r u", j=count, u=2),
         )
 
@@ -55,9 +64,9 @@ def tile_tsh_mid_block_pb_t_kernel(tc, h, w_f2, b_f2, res1, g2, be2, w_h, b_h, o
 
     with ExitStack() as ctx:
         const = ctx.enter_context(tc.tile_pool(name="const", bufs=1))
-        loads = ctx.enter_context(tc.tile_pool(name="loads", bufs=5))
+        loads = ctx.enter_context(tc.tile_pool(name="loads", bufs=4))
         work = ctx.enter_context(tc.tile_pool(name="work", bufs=3))
-        ahead = ctx.enter_context(tc.tile_pool(name="ahead", bufs=5))
+        ahead = ctx.enter_context(tc.tile_pool(name="ahead", bufs=4))
         bias_bank = ctx.enter_context(tc.psum_pool(name="bias_bank", bufs=1))
         ring = ctx.enter_context(tc.psum_pool(name="ring", bufs=7))
 
@@ -66,6 +75,7 @@ def tile_tsh_mid_block_pb_t_kernel(tc, h, w_f2, b_f2, res1, g2, be2, w_h, b_h, o
 
         ident = const.tile([P, P], F32)
         make_identity(nc, ident[:])
+        ident_bf16 = const.tile([P, P], BF16)
         eps = const.tile([P, 1], F32)
         nc.vector.memset(eps[:], LN_EPS)
         bias_rows = const.tile([P, MID + D_OUT], BF16)
@@ -74,6 +84,7 @@ def tile_tsh_mid_block_pb_t_kernel(tc, h, w_f2, b_f2, res1, g2, be2, w_h, b_h, o
         nc.vector.memset(ones[:], 1.0)
         vec_rows = const.tile([P, MID], BF16)
         nc.vector.memset(vec_rows[:], 0.0)
+        nc.vector.tensor_copy(out=ident_bf16[:], in_=ident[:])
         table_warm = const.tile([P, 1], F32)
         nc.scalar.activation(out=table_warm[:], in_=eps[:], func=ACT.Abs_reciprocal_sqrt)
 
@@ -105,12 +116,15 @@ def tile_tsh_mid_block_pb_t_kernel(tc, h, w_f2, b_f2, res1, g2, be2, w_h, b_h, o
             nc.sync.dma_start(out=w2_sb[:], in_=w_h.rearrange("(r p) m -> p r m", p=P))
 
         def prepare_first_weights():
+            banks = transpose_words(nc, new_bank, w1_sb[:], ident[:])
+            group_words(banks, w1_grouped[:], [nc.scalar.copy, nc.vector.tensor_copy])
+            nc.vector.quantize_mx(out=w1_codes[:].bitcast(FP8X4), scales=w1_scales[:], in_=w1_grouped[:])
+
+        def spread_first_bias():
             for t in range(PACK):
                 nc.tensor.matmul(
                     out=b1_all[:, t * P : (t + 1) * P], lhsT=ones[:], rhs=bias_rows[:, t:MID:PACK], start=True, stop=True
                 )
-            transpose_bf16_rows(nc, new_bank, w1_grouped[:], w1_sb[:], ident[:], [nc.scalar.copy, nc.vector.tensor_copy])
-            nc.vector.quantize_mx(out=w1_codes[:].bitcast(FP8X4), scales=w1_scales[:], in_=w1_grouped[:])
 
         def prepare_last_weights():
             b2_spread = new_bank()
@@ -125,14 +139,14 @@ def tile_tsh_mid_block_pb_t_kernel(tc, h, w_f2, b_f2, res1, g2, be2, w_h, b_h, o
             for t in range(PACK):
                 nc.tensor.transpose(vec_t[:, t * P : (t + 1) * P], vec_rows_f32[:, t:MID:PACK], ident[:])
             nc.scalar.copy(out=vec_cols[:], in_=vec_t[:].rearrange("p (t v) -> p t v", t=PACK)[:, :, 0:2])
-            transpose_bf16_rows(nc, new_bank, w2_grouped[:], w2_sb[:], ident[:], [nc.scalar.copy])
+            group_words(transpose_words(nc, new_bank, w2_sb[:], ident[:]), w2_grouped[:], [nc.scalar.copy])
 
         def quantise_last_weight():
             nc.vector.quantize_mx(out=w2_codes[:].bitcast(FP8X4), scales=w2_scales[:], in_=w2_grouped[:])
 
-        h_in, res_in, h_grouped, h_packed = {}, {}, {}, {}
-        res_biased, res2_of, sums_of, neg_mean_of, rstd_of, normed_of = {}, {}, {}, {}, {}, {}
-        n_planes, n_grouped, n_packed = {}, {}, {}
+        h_in, res_in, h_pairs, h_grouped, h_packed = {}, {}, {}, {}, {}
+        ffn_of, biased_of, res_biased, res2_of, sums_of, square_sums_of = {}, {}, {}, {}, {}, {}
+        neg_mean_of, rstd_of, normed_of, chunks_of, n_planes, n_grouped, n_packed = {}, {}, {}, {}, {}, {}, {}
 
         def load(g):
             n, first = SIZES[g], STARTS[g]
@@ -143,20 +157,41 @@ def tile_tsh_mid_block_pb_t_kernel(tc, h, w_f2, b_f2, res1, g2, be2, w_h, b_h, o
             h_in[g], res_in[g] = h_sb, res_sb
 
         def transpose_h(g):
+            h_pairs[g] = transpose_words(nc, new_bank, h_in[g][:], ident[:])
+
+        def group_h(g):
             grouped = work.tile([P, SIZES[g] * FFN], BF16, align_bytes=64)
-            transpose_bf16_rows(nc, new_bank, grouped[:], h_in[g][:], ident[:], [nc.scalar.copy])
+            group_words(h_pairs[g], grouped[:], [nc.scalar.copy])
             h_grouped[g] = grouped
 
-        def bias_residual(g):
-            n = SIZES[g]
-            res_b = ahead.tile([P, n, MID], F32)
+        def on_tensor(g, j):
+            return j == 3
+
+        def add_bias_on_tensor(g):
+            res_biased[g] = ahead.tile([P, SIZES[g], MID], F32, name="res_b")
+            for j in range(SIZES[g]):
+                if on_tensor(g, j):
+                    biased = new_bank()
+                    nc.tensor.matmul(out=biased[:], lhsT=ident_bf16[:], rhs=res_in[g][:, j, :], start=True, stop=False)
+                    nc.tensor.matmul(out=biased[:], lhsT=ones[:], rhs=bias_rows[:, 0:MID], start=False, stop=True)
+                    biased_of[g] = biased
+
+        def copy_biased(g):
+            for j in range(SIZES[g]):
+                if on_tensor(g, j):
+                    nc.scalar.copy(
+                        out=res_biased[g][:, j, :].rearrange("p (t m) -> p t m", t=PACK),
+                        in_=biased_of[g][:].rearrange("p (m t) -> p t m", t=PACK),
+                    )
+
+        def add_bias(g):
+            n = sum(not on_tensor(g, j) for j in range(SIZES[g]))
             nc.vector.tensor_tensor(
-                out=res_b[:].rearrange("p j (t m) -> p j t m", t=PACK),
-                in0=res_in[g][:].rearrange("p j (m t) -> p j t m", t=PACK),
+                out=res_biased[g][:, 0:n, :].rearrange("p j (t m) -> p j t m", t=PACK),
+                in0=res_in[g][:, 0:n, :].rearrange("p j (m t) -> p j t m", t=PACK),
                 in1=b1_all[:].rearrange("p (t m) -> p t m", t=PACK).unsqueeze(1).to_broadcast([P, n, PACK, P]),
                 op=ADD,
             )
-            res_biased[g] = res_b
 
         def quantise_h(g):
             h_codes = work.tile([P, SIZES[g] * P], U32, align_bytes=64)
@@ -165,11 +200,9 @@ def tile_tsh_mid_block_pb_t_kernel(tc, h, w_f2, b_f2, res1, g2, be2, w_h, b_h, o
             h_packed[g] = (h_codes, h_scales)
 
         def first_matmul(g):
-            n = SIZES[g]
             h_codes, h_scales = h_packed[g]
-            res2 = work.tile([P, n, MID], F32)
-            sums = work.tile([P, n], F32)
-            for j in range(n):
+            ffn_of[g] = []
+            for j in range(SIZES[g]):
                 tokens = slice(j * P, (j + 1) * P)
                 ffn = new_bank()
                 nc.tensor.matmul_mx(
@@ -181,75 +214,86 @@ def tile_tsh_mid_block_pb_t_kernel(tc, h, w_f2, b_f2, res1, g2, be2, w_h, b_h, o
                     start=True,
                     stop=True,
                 )
-                nc.vector.scalar_tensor_tensor(
-                    out=res2[:, j, :], in0=ffn[:], scalar=1.0, in1=res_biased[g][:, j, :], op0=MULT, op1=ADD,
-                    accum_out=sums[:, j : j + 1],
-                )
-            res2_of[g], sums_of[g] = res2, sums
+                ffn_of[g].append(ffn)
 
-        def statistics(g):
+        def add_residual(g, tiles):
             n = SIZES[g]
-            neg_mean = work.tile([P, n], F32)
-            nc.scalar.mul(out=neg_mean[:], in_=sums_of[g][:], mul=-1.0 / MID)
-            squares = work.tile([P, n, MID], BF16)
+            if g not in res2_of:
+                res2_of[g] = work.tile([P, n, MID], F32, name="res2")
+                sums_of[g] = work.tile([P, n], F32, name="sums")
+            for j in tiles:
+                if j < n:
+                    nc.vector.scalar_tensor_tensor(
+                        out=res2_of[g][:, j, :], in0=ffn_of[g][j][:], scalar=1.0, in1=res_biased[g][:, j, :],
+                        op0=MULT, op1=ADD, accum_out=sums_of[g][:, j : j + 1],
+                    )
+
+        def squares(g):
+            n = SIZES[g]
+            ignored = work.tile([P, n, MID], BF16)
             square_sums = work.tile([P, n], F32)
             for j in range(n):
                 nc.scalar.activation(
-                    out=squares[:, j, :], in_=res2_of[g][:, j, :], func=ACT.Square,
-                    bias=neg_mean[:, j : j + 1], scale=1.0, accum_out=square_sums[:, j : j + 1],
+                    out=ignored[:, j, :], in_=res2_of[g][:, j, :], func=ACT.Square,
+                    bias=sums_of[g][:, j : j + 1], scale=-float(MID), accum_out=square_sums[:, j : j + 1],
                 )
-            rstd = work.tile([P, n], F32)
-            nc.scalar.activation(
-                out=rstd[:], in_=square_sums[:], func=ACT.Abs_reciprocal_sqrt, scale=1.0 / MID, bias=eps[:, 0:1]
-            )
-            neg_mean_of[g], rstd_of[g] = neg_mean, rstd
+            square_sums_of[g] = square_sums
 
-        def on_scalar(g, j):
-            return g % 2 == 1 and j == 1
+        def negative_mean(g):
+            neg_mean = work.tile([P, SIZES[g]], F32)
+            nc.scalar.mul(out=neg_mean[:], in_=sums_of[g][:], mul=-1.0 / MID)
+            neg_mean_of[g] = neg_mean
+
+        def reciprocal_deviation(g):
+            rstd = work.tile([P, SIZES[g]], F32)
+            nc.scalar.activation(
+                out=rstd[:], in_=square_sums_of[g][:], func=ACT.Abs_reciprocal_sqrt, scale=1.0 / MID**3, bias=eps[:, 0:1]
+            )
+            rstd_of[g] = rstd
+
+        def gpsimd_or_vector(g):
+            return nc.vector if g >= GROUPS - VECTOR_GROUPS else nc.gpsimd
 
         def normalise(g):
             n = SIZES[g]
             normed = work.tile([P, n, MID], F32)
             for j in range(n):
-                neg_mean, rstd = neg_mean_of[g][:, j : j + 1], rstd_of[g][:, j : j + 1]
-                if on_scalar(g, j):
-                    offset = work.tile([P, 1], F32)
-                    nc.scalar.activation(out=offset[:], in_=neg_mean, func=ACT.Identity, scale=rstd)
-                    nc.scalar.activation(
-                        out=normed[:, j, :], in_=res2_of[g][:, j, :], func=ACT.Identity, scale=rstd, bias=offset[:]
-                    )
-                else:
-                    nc.gpsimd.tensor_scalar(
-                        out=normed[:, j, :], in0=res2_of[g][:, j, :], scalar1=neg_mean, scalar2=rstd, op0=ADD, op1=MULT
-                    )
+                gpsimd_or_vector(g).tensor_scalar(
+                    out=normed[:, j, :], in0=res2_of[g][:, j, :], scalar1=neg_mean_of[g][:, j : j + 1],
+                    scalar2=rstd_of[g][:, j : j + 1], op0=ADD, op1=MULT,
+                )
             normed_of[g] = normed
 
         def transpose_norm(g):
             n = SIZES[g]
-            planes = work.tile([P, PACK, n * P], BF16)
-            for half in range(2):
-                chunks = new_bank()
-                for e in range(2):
-                    t = 2 * half + e
-                    for j in range(n):
-                        nc.tensor.transpose(
-                            chunks[:, (e * n + j) * P : (e * n + j + 1) * P], normed_of[g][:, j, t * P : (t + 1) * P], ident[:]
-                        )
-                for e in range(2):
-                    t = 2 * half + e
-                    nc.scalar.activation(
-                        out=planes[:, t, :], in_=chunks[:, e * n * P : (e + 1) * n * P], func=ACT.Identity,
-                        scale=gain[t], bias=shift[t],
+            chunks_of[g] = []
+            for t in range(PACK):
+                if t % (PACK // n) == 0:
+                    chunks = new_bank()
+                first = t % (PACK // n) * n
+                for j in range(n):
+                    nc.tensor.transpose(
+                        chunks[:, (first + j) * P : (first + j + 1) * P], normed_of[g][:, j, t * P : (t + 1) * P], ident[:]
                     )
-            n_planes[g] = planes
+                chunks_of[g].append(chunks[:, first * P : (first + n) * P])
+            n_planes[g] = work.tile([P, PACK, n * P], BF16, name="planes")
+
+        def scale_and_shift(g, ts):
+            for t in ts:
+                nc.scalar.activation(
+                    out=n_planes[g][:, t, :], in_=chunks_of[g][t], func=ACT.Identity, scale=gain[t], bias=shift[t]
+                )
 
         def group_norm(g):
-            grouped = work.tile([P, SIZES[g] * P * PACK], BF16, align_bytes=64)
-            nc.gpsimd.tensor_scalar(
-                out=grouped[:].rearrange("p (w t) -> p w t", t=PACK),
-                in0=n_planes[g][:].rearrange("p t w -> p w t"),
-                scalar1=1.0, scalar2=0.0, op0=MULT, op1=ADD,
-            )
+            n = SIZES[g]
+            grouped = work.tile([P, n * P * PACK], BF16, align_bytes=64)
+            for first in range(0, n, 2):
+                tokens = slice(first * P, min(first + 2, n) * P)
+                gpsimd_or_vector(g).tensor_scalar(
+                    out=grouped[:].rearrange("p (w t) -> p w t", t=PACK)[:, tokens, :],
+                    in0=n_planes[g][:, :, tokens].rearrange("p t w -> p w t"),
+                    scalar1=1.0, scalar2=0.0, op0=MULT, op1=ADD,
+                )
             n_grouped[g] = grouped
 
         def quantise_norm(g):
@@ -262,24 +306,26 @@ def tile_tsh_mid_block_pb_t_kernel(tc, h, w_f2, b_f2, res1, g2, be2, w_h, b_h, o
             n, first = SIZES[g], STARTS[g]
             n_codes, n_scales = n_packed[g]
             result = work.tile([P, n, D_OUT], F32)
-            head = new_bank()
-            for j in range(n):
-                tokens = slice(j * P, (j + 1) * P)
-                nc.tensor.matmul_mx(
-                    out=head[:, j * D_OUT : (j + 1) * D_OUT],
-                    lhsT=n_codes[:, tokens].bitcast(FP8X4),
-                    lhsT_scale=n_scales[:, tokens],
-                    rhs=w2_codes[:].bitcast(FP8X4),
-                    rhs_scale=w2_scales[:],
-                    start=True,
-                    stop=True,
+            for b in range(0, n, 2):
+                count = min(2, n - b)
+                head = new_bank()
+                for j in range(count):
+                    tokens = slice((b + j) * P, (b + j + 1) * P)
+                    nc.tensor.matmul_mx(
+                        out=head[:, j * D_OUT : (j + 1) * D_OUT],
+                        lhsT=n_codes[:, tokens].bitcast(FP8X4),
+                        lhsT_scale=n_scales[:, tokens],
+                        rhs=w2_codes[:].bitcast(FP8X4),
+                        rhs_scale=w2_scales[:],
+                        start=True,
+                        stop=True,
+                    )
+                nc.vector.tensor_tensor(
+                    out=result[:, b : b + count, :],
+                    in0=head[:, 0 : count * D_OUT].rearrange("p (j o) -> p j o", j=count),
+                    in1=b2_all[:].unsqueeze(1).to_broadcast([P, count, D_OUT]),
+                    op=ADD,
                 )
-            nc.vector.tensor_tensor(
-                out=result[:],
-                in0=head[:, 0 : n * D_OUT].rearrange("p (j o) -> p j o", j=n),
-                in1=b2_all[:].unsqueeze(1).to_broadcast([P, n, D_OUT]),
-                op=ADD,
-            )
             nc.sync.dma_start(out=out_rows[:, first : first + n, :], in_=result[:])
 
         def live(g):
@@ -288,32 +334,51 @@ def tile_tsh_mid_block_pb_t_kernel(tc, h, w_f2, b_f2, res1, g2, be2, w_h, b_h, o
         with tc.manual_schedule():
             load_first_weights()
             for k in range(GROUPS + 7):
-                if live(k - 5):
-                    statistics(k - 5)
-                if k == 2:
-                    prepare_first_weights()
-                if live(k - 2):
-                    transpose_h(k - 2)
-                if k == 3:
-                    prepare_last_weights()
-                if live(k - 5):
-                    normalise(k - 5)
-                if live(k - 6):
-                    transpose_norm(k - 6)
-                if live(k - 2):
-                    bias_residual(k - 2)
-                if live(k - 3):
-                    quantise_h(k - 3)
-                if live(k - 7):
-                    quantise_norm(k - 7)
                 if live(k):
                     load(k)
                 if k == 1:
                     load_last_weights()
+                if live(k - 5):
+                    squares(k - 5)
+                    negative_mean(k - 5)
+                if k == 2:
+                    prepare_first_weights()
+                if live(k - 2):
+                    transpose_h(k - 2)
+                if k == 2:
+                    spread_first_bias()
+                if live(k - 6):
+                    transpose_norm(k - 6)
+                    scale_and_shift(k - 6, [0])
+                if live(k - 5):
+                    reciprocal_deviation(k - 5)
+                if live(k - 6):
+                    scale_and_shift(k - 6, [1])
+                if live(k - 6):
+                    scale_and_shift(k - 6, [2, 3])
+                if live(k - 2):
+                    group_h(k - 2)
+                if k == 3:
+                    prepare_last_weights()
+                if live(k - 2):
+                    add_bias_on_tensor(k - 2)
+                    add_bias(k - 2)
                 if live(k - 4):
                     first_matmul(k - 4)
+                if live(k - 3):
+                    quantise_h(k - 3)
+                if live(k - 2):
+                    copy_biased(k - 2)
+                if live(k - 4):
+                    add_residual(k - 4, (0, 1))
+                if live(k - 7):
+                    quantise_norm(k - 7)
+                if live(k - 4):
+                    add_residual(k - 4, (2, 3))
                 if k == 5:
                     quantise_last_weight()
+                if live(k - 5):
+                    normalise(k - 5)
                 if live(k - 6):
                     group_norm(k - 6)
                 if live(k - 7):

@@ -13,6 +13,7 @@ MULT = mybir.AluOpType.mult
 ACT = mybir.ActivationFunctionType
 
 P = 128
+RUN = 4
 PACK = 4
 BANK = 512
 TOKENS = 8 * 1024
@@ -144,7 +145,7 @@ def tile_tsh_mid_block_pb_t_kernel(tc, h, w_f2, b_f2, res1, g2, be2, w_h, b_h, o
         def quantise_last_weight():
             nc.vector.quantize_mx(out=w2_codes[:].bitcast(FP8X4), scales=w2_scales[:], in_=w2_grouped[:])
 
-        h_in, res_in, h_pairs, h_grouped, h_packed = {}, {}, {}, {}, {}
+        h_in, res_in, h_pairs, grouped_of, h_packed = {}, {}, {}, {}, {}
         ffn_of, biased_of, res_biased, res2_of, sums_of, square_sums_of = {}, {}, {}, {}, {}, {}
         neg_mean_of, rstd_of, normed_of, chunks_of, n_planes, n_grouped, n_packed = {}, {}, {}, {}, {}, {}, {}
 
@@ -159,10 +160,16 @@ def tile_tsh_mid_block_pb_t_kernel(tc, h, w_f2, b_f2, res1, g2, be2, w_h, b_h, o
         def transpose_h(g):
             h_pairs[g] = transpose_words(nc, new_bank, h_in[g][:], ident[:])
 
+        def mate(g):
+            return g >= 4 and g < GROUPS and SIZES[g] == SIZES[g - 4]
+
         def group_h(g):
-            grouped = work.tile([P, SIZES[g] * FFN], BF16, align_bytes=64)
-            group_words(h_pairs[g], grouped[:], [nc.scalar.copy])
-            h_grouped[g] = grouped
+            width = SIZES[g] * FFN
+            grouped = work.tile([P, 2 * width if mate(g) else width], BF16, align_bytes=64)
+            group_words(h_pairs[g], grouped[:, 0:width], [nc.scalar.copy])
+            grouped_of[g] = grouped
+            if mate(g):
+                n_grouped[g - 4] = grouped[:, width : 2 * width]
 
         def on_tensor(g, j):
             return j == 3
@@ -194,10 +201,14 @@ def tile_tsh_mid_block_pb_t_kernel(tc, h, w_f2, b_f2, res1, g2, be2, w_h, b_h, o
             )
 
         def quantise_h(g):
-            h_codes = work.tile([P, SIZES[g] * P], U32, align_bytes=64)
-            h_scales = work.tile([P, SIZES[g] * P], U8, align_bytes=64)
-            nc.vector.quantize_mx(out=h_codes[:].bitcast(FP8X4), scales=h_scales[:], in_=h_grouped[g][:])
-            h_packed[g] = (h_codes, h_scales)
+            width = SIZES[g] * P
+            columns = 2 * width if mate(g) else width
+            codes = work.tile([P, columns], U32, align_bytes=64)
+            scales = work.tile([P, columns], U8, align_bytes=64)
+            nc.vector.quantize_mx(out=codes[:].bitcast(FP8X4), scales=scales[:], in_=grouped_of[g][:])
+            h_packed[g] = (codes[:, 0:width], scales[:, 0:width])
+            if mate(g):
+                n_packed[g - 4] = (codes[:, width : 2 * width], scales[:, width : 2 * width])
 
         def first_matmul(g):
             h_codes, h_scales = h_packed[g]
@@ -216,17 +227,15 @@ def tile_tsh_mid_block_pb_t_kernel(tc, h, w_f2, b_f2, res1, g2, be2, w_h, b_h, o
                 )
                 ffn_of[g].append(ffn)
 
-        def add_residual(g, tiles):
+        def add_residual(g):
             n = SIZES[g]
-            if g not in res2_of:
-                res2_of[g] = work.tile([P, n, MID], F32, name="res2")
-                sums_of[g] = work.tile([P, n], F32, name="sums")
-            for j in tiles:
-                if j < n:
-                    nc.vector.scalar_tensor_tensor(
-                        out=res2_of[g][:, j, :], in0=ffn_of[g][j][:], scalar=1.0, in1=res_biased[g][:, j, :],
-                        op0=MULT, op1=ADD, accum_out=sums_of[g][:, j : j + 1],
-                    )
+            res2_of[g] = work.tile([P, n, MID], F32, name="res2")
+            sums_of[g] = work.tile([P, n], F32, name="sums")
+            for j in range(n):
+                nc.vector.scalar_tensor_tensor(
+                    out=res2_of[g][:, j, :], in0=ffn_of[g][j][:], scalar=1.0, in1=res_biased[g][:, j, :],
+                    op0=MULT, op1=ADD, accum_out=sums_of[g][:, j : j + 1],
+                )
 
         def squares(g):
             n = SIZES[g]
@@ -251,14 +260,14 @@ def tile_tsh_mid_block_pb_t_kernel(tc, h, w_f2, b_f2, res1, g2, be2, w_h, b_h, o
             )
             rstd_of[g] = rstd
 
-        def gpsimd_or_vector(g):
-            return nc.vector if g >= GROUPS - VECTOR_GROUPS else nc.gpsimd
+        def last(g):
+            return g >= GROUPS - VECTOR_GROUPS
 
         def normalise(g):
-            n = SIZES[g]
-            normed = work.tile([P, n, MID], F32)
-            for j in range(n):
-                gpsimd_or_vector(g).tensor_scalar(
+            normed = work.tile([P, SIZES[g], MID], F32)
+            for j in range(SIZES[g]):
+                engine = nc.vector if j == 3 or last(g) else nc.gpsimd
+                engine.tensor_scalar(
                     out=normed[:, j, :], in0=res2_of[g][:, j, :], scalar1=neg_mean_of[g][:, j : j + 1],
                     scalar2=rstd_of[g][:, j : j + 1], op0=ADD, op1=MULT,
                 )
@@ -286,21 +295,25 @@ def tile_tsh_mid_block_pb_t_kernel(tc, h, w_f2, b_f2, res1, g2, be2, w_h, b_h, o
 
         def group_norm(g):
             n = SIZES[g]
-            grouped = work.tile([P, n * P * PACK], BF16, align_bytes=64)
+            if not mate(g + 4):
+                own = work.tile([P, n * P * PACK], BF16, align_bytes=64)
+                n_grouped[g] = own[:]
+            grouped = n_grouped[g]
             for first in range(0, n, 2):
                 tokens = slice(first * P, min(first + 2, n) * P)
-                gpsimd_or_vector(g).tensor_scalar(
-                    out=grouped[:].rearrange("p (w t) -> p w t", t=PACK)[:, tokens, :],
-                    in0=n_planes[g][:, :, tokens].rearrange("p t w -> p w t"),
+                engine = nc.vector if last(g) else nc.gpsimd
+                engine.tensor_scalar(
+                    out=grouped[:, tokens.start * PACK : tokens.stop * PACK].rearrange("p (w i t) -> p w t i", i=RUN, t=PACK),
+                    in0=n_planes[g][:, :, tokens].rearrange("p t (w i) -> p w t i", i=RUN),
                     scalar1=1.0, scalar2=0.0, op0=MULT, op1=ADD,
                 )
-            n_grouped[g] = grouped
 
         def quantise_norm(g):
-            n_codes = work.tile([P, SIZES[g] * P], U32, align_bytes=64)
-            n_scales = work.tile([P, SIZES[g] * P], U8, align_bytes=64)
-            nc.vector.quantize_mx(out=n_codes[:].bitcast(FP8X4), scales=n_scales[:], in_=n_grouped[g][:])
-            n_packed[g] = (n_codes, n_scales)
+            if not mate(g + 4):
+                n_codes = work.tile([P, SIZES[g] * P], U32, align_bytes=64)
+                n_scales = work.tile([P, SIZES[g] * P], U8, align_bytes=64)
+                nc.vector.quantize_mx(out=n_codes[:].bitcast(FP8X4), scales=n_scales[:], in_=n_grouped[g])
+                n_packed[g] = (n_codes[:], n_scales[:])
 
         def second_matmul(g):
             n, first = SIZES[g], STARTS[g]
@@ -347,6 +360,8 @@ def tile_tsh_mid_block_pb_t_kernel(tc, h, w_f2, b_f2, res1, g2, be2, w_h, b_h, o
                     transpose_h(k - 2)
                 if k == 2:
                     spread_first_bias()
+                if live(k - 4) and last(k - 4):
+                    first_matmul(k - 4)
                 if live(k - 6):
                     transpose_norm(k - 6)
                     scale_and_shift(k - 6, [0])
@@ -363,22 +378,24 @@ def tile_tsh_mid_block_pb_t_kernel(tc, h, w_f2, b_f2, res1, g2, be2, w_h, b_h, o
                 if live(k - 2):
                     add_bias_on_tensor(k - 2)
                     add_bias(k - 2)
-                if live(k - 4):
+                if live(k - 4) and not last(k - 4):
                     first_matmul(k - 4)
                 if live(k - 3):
                     quantise_h(k - 3)
-                if live(k - 2):
-                    copy_biased(k - 2)
-                if live(k - 4):
-                    add_residual(k - 4, (0, 1))
+                if live(k - 4) and last(k - 4):
+                    add_residual(k - 4)
                 if live(k - 7):
                     quantise_norm(k - 7)
-                if live(k - 4):
-                    add_residual(k - 4, (2, 3))
+                if live(k - 5) and not last(k - 5):
+                    normalise(k - 5)
+                if live(k - 2):
+                    copy_biased(k - 2)
+                if live(k - 4) and not last(k - 4):
+                    add_residual(k - 4)
+                if live(k - 5) and last(k - 5):
+                    normalise(k - 5)
                 if k == 5:
                     quantise_last_weight()
-                if live(k - 5):
-                    normalise(k - 5)
                 if live(k - 6):
                     group_norm(k - 6)
                 if live(k - 7):

@@ -21,6 +21,7 @@ FFN = 512
 MID = 512
 D_OUT = 256
 LN_EPS = 1e-5
+WARM_TURNS = 5
 TILES = TOKENS // P
 SIZES = [1, 1, 2] + [4] * (TILES // 4 - 2) + [2, 1, 1]
 VECTOR_GROUPS = 3
@@ -83,6 +84,8 @@ def tile_tsh_mid_block_pb_t_kernel(tc, h, w_f2, b_f2, res1, g2, be2, w_h, b_h, o
         nc.vector.memset(bias_rows[:], 0.0)
         ones = const.tile([P, P], BF16)
         nc.vector.memset(ones[:], 1.0)
+        zeros = const.tile([P, BANK], BF16)
+        nc.vector.memset(zeros[:], 0.0)
         vec_rows = const.tile([P, MID], BF16)
         nc.vector.memset(vec_rows[:], 0.0)
         nc.vector.tensor_copy(out=ident_bf16[:], in_=ident[:])
@@ -103,6 +106,11 @@ def tile_tsh_mid_block_pb_t_kernel(tc, h, w_f2, b_f2, res1, g2, be2, w_h, b_h, o
         w2_grouped = const.tile([P, D_OUT // P * MID], BF16, align_bytes=64)
         w2_codes = const.tile([P, D_OUT], U32, align_bytes=64)
         w2_scales = const.tile([P, D_OUT], U8, align_bytes=64)
+
+        def warm_tensor():
+            unread = new_bank()
+            for turn in range(WARM_TURNS):
+                nc.tensor.matmul(out=unread[:], lhsT=ones[:], rhs=zeros[:], start=True, stop=True)
 
         def load_first_weights():
             w_rows = w_f2.rearrange("(m t) k -> m t k", t=PACK)
@@ -294,19 +302,15 @@ def tile_tsh_mid_block_pb_t_kernel(tc, h, w_f2, b_f2, res1, g2, be2, w_h, b_h, o
                 )
 
         def group_norm(g):
-            n = SIZES[g]
             if not mate(g + 4):
-                own = work.tile([P, n * P * PACK], BF16, align_bytes=64)
+                own = work.tile([P, SIZES[g] * P * PACK], BF16, align_bytes=64)
                 n_grouped[g] = own[:]
-            grouped = n_grouped[g]
-            for first in range(0, n, 2):
-                tokens = slice(first * P, min(first + 2, n) * P)
-                engine = nc.vector if last(g) else nc.gpsimd
-                engine.tensor_scalar(
-                    out=grouped[:, tokens.start * PACK : tokens.stop * PACK].rearrange("p (w i t) -> p w t i", i=RUN, t=PACK),
-                    in0=n_planes[g][:, :, tokens].rearrange("p t (w i) -> p w t i", i=RUN),
-                    scalar1=1.0, scalar2=0.0, op0=MULT, op1=ADD,
-                )
+            engine = nc.vector if last(g) else nc.gpsimd
+            engine.tensor_scalar(
+                out=n_grouped[g].rearrange("p (w i t) -> p w t i", i=RUN, t=PACK),
+                in0=n_planes[g][:].rearrange("p t (w i) -> p w t i", i=RUN),
+                scalar1=1.0, scalar2=0.0, op0=MULT, op1=ADD,
+            )
 
         def quantise_norm(g):
             if not mate(g + 4):
@@ -346,6 +350,7 @@ def tile_tsh_mid_block_pb_t_kernel(tc, h, w_f2, b_f2, res1, g2, be2, w_h, b_h, o
 
         with tc.manual_schedule():
             load_first_weights()
+            warm_tensor()
             for k in range(GROUPS + 7):
                 if live(k):
                     load(k)

@@ -13,7 +13,6 @@ MULT = mybir.AluOpType.mult
 ACT = mybir.ActivationFunctionType
 
 P = 128
-RUN = 4
 PACK = 4
 BANK = 512
 TOKENS = 8 * 1024
@@ -21,7 +20,6 @@ FFN = 512
 MID = 512
 D_OUT = 256
 LN_EPS = 1e-5
-WARM_TURNS = 5
 TILES = TOKENS // P
 SIZES = [1, 1, 2] + [4] * (TILES // 4 - 2) + [2, 1, 1]
 VECTOR_GROUPS = 3
@@ -84,8 +82,6 @@ def tile_tsh_mid_block_pb_t_kernel(tc, h, w_f2, b_f2, res1, g2, be2, w_h, b_h, o
         nc.vector.memset(bias_rows[:], 0.0)
         ones = const.tile([P, P], BF16)
         nc.vector.memset(ones[:], 1.0)
-        zeros = const.tile([P, BANK], BF16)
-        nc.vector.memset(zeros[:], 0.0)
         vec_rows = const.tile([P, MID], BF16)
         nc.vector.memset(vec_rows[:], 0.0)
         nc.vector.tensor_copy(out=ident_bf16[:], in_=ident[:])
@@ -106,11 +102,6 @@ def tile_tsh_mid_block_pb_t_kernel(tc, h, w_f2, b_f2, res1, g2, be2, w_h, b_h, o
         w2_grouped = const.tile([P, D_OUT // P * MID], BF16, align_bytes=64)
         w2_codes = const.tile([P, D_OUT], U32, align_bytes=64)
         w2_scales = const.tile([P, D_OUT], U8, align_bytes=64)
-
-        def warm_tensor():
-            unread = new_bank()
-            for turn in range(WARM_TURNS):
-                nc.tensor.matmul(out=unread[:], lhsT=ones[:], rhs=zeros[:], start=True, stop=True)
 
         def load_first_weights():
             w_rows = w_f2.rearrange("(m t) k -> m t k", t=PACK)
@@ -180,7 +171,7 @@ def tile_tsh_mid_block_pb_t_kernel(tc, h, w_f2, b_f2, res1, g2, be2, w_h, b_h, o
                 n_grouped[g - 4] = grouped[:, width : 2 * width]
 
         def on_tensor(g, j):
-            return j == 3
+            return j > 0 and j == SIZES[g] - 1
 
         def add_bias_on_tensor(g):
             res_biased[g] = ahead.tile([P, SIZES[g], MID], F32, name="res_b")
@@ -274,7 +265,7 @@ def tile_tsh_mid_block_pb_t_kernel(tc, h, w_f2, b_f2, res1, g2, be2, w_h, b_h, o
         def normalise(g):
             normed = work.tile([P, SIZES[g], MID], F32)
             for j in range(SIZES[g]):
-                engine = nc.vector if j == 3 or last(g) else nc.gpsimd
+                engine = nc.vector if (j == 3 and g % 2 == 0) or last(g) else nc.gpsimd
                 engine.tensor_scalar(
                     out=normed[:, j, :], in0=res2_of[g][:, j, :], scalar1=neg_mean_of[g][:, j : j + 1],
                     scalar2=rstd_of[g][:, j : j + 1], op0=ADD, op1=MULT,
@@ -307,8 +298,8 @@ def tile_tsh_mid_block_pb_t_kernel(tc, h, w_f2, b_f2, res1, g2, be2, w_h, b_h, o
                 n_grouped[g] = own[:]
             engine = nc.vector if last(g) else nc.gpsimd
             engine.tensor_scalar(
-                out=n_grouped[g].rearrange("p (w i t) -> p w t i", i=RUN, t=PACK),
-                in0=n_planes[g][:].rearrange("p t (w i) -> p w t i", i=RUN),
+                out=n_grouped[g].rearrange("p (w t) -> p w t", t=PACK),
+                in0=n_planes[g][:].rearrange("p t w -> p w t"),
                 scalar1=1.0, scalar2=0.0, op0=MULT, op1=ADD,
             )
 
@@ -350,7 +341,6 @@ def tile_tsh_mid_block_pb_t_kernel(tc, h, w_f2, b_f2, res1, g2, be2, w_h, b_h, o
 
         with tc.manual_schedule():
             load_first_weights()
-            warm_tensor()
             for k in range(GROUPS + 7):
                 if live(k):
                     load(k)

@@ -13,6 +13,7 @@ MULT = mybir.AluOpType.mult
 ACT = mybir.ActivationFunctionType
 
 P = 128
+RUN = 4
 PACK = 4
 BANK = 512
 TOKENS = 8 * 1024
@@ -298,8 +299,8 @@ def tile_tsh_mid_block_pb_t_kernel(tc, h, w_f2, b_f2, res1, g2, be2, w_h, b_h, o
                 n_grouped[g] = own[:]
             engine = nc.vector if last(g) else nc.gpsimd
             engine.tensor_scalar(
-                out=n_grouped[g].rearrange("p (w t) -> p w t", t=PACK),
-                in0=n_planes[g][:].rearrange("p t w -> p w t"),
+                out=n_grouped[g].rearrange("p (w i t) -> p w t i", i=RUN, t=PACK),
+                in0=n_planes[g][:].rearrange("p t (w i) -> p w t i", i=RUN),
                 scalar1=1.0, scalar2=0.0, op0=MULT, op1=ADD,
             )
 

from contextlib import ExitStack

import concourse.mybir as mybir
from concourse.masks import make_identity

F32 = mybir.dt.float32
BF16 = mybir.dt.bfloat16
U32 = mybir.dt.uint32
U8 = mybir.dt.uint8
FP8X4 = mybir.dt.float8_e4m3fn_x4
ADD = mybir.AluOpType.add
MULT = mybir.AluOpType.mult
ACT = mybir.ActivationFunctionType

P = 128
RUN = 4
PACK = 4
BANK = 512
TOKENS = 8 * 1024
FFN = 512
MID = 512
D_OUT = 256
LN_EPS = 1e-5
TILES = TOKENS // P
SIZES = [1, 1, 2] + [4] * (TILES // 4 - 2) + [2, 1, 1]
VECTOR_GROUPS = 3
STARTS = [sum(SIZES[:g]) for g in range(len(SIZES))]
GROUPS = len(SIZES)

FLOPS = 2 * TOKENS * FFN * MID + 2 * TOKENS * MID * D_OUT


def transpose_words(nc, new_bank, rows, ident):
    n = rows.shape[1]
    words = rows.rearrange("p n k -> p (n k)").bitcast(F32)
    banks = []
    for first in range(0, n, 2):
        pairs_t = new_bank()
        for j in range(min(2, n - first)):
            word = (first + j) * 2 * P
            for u in range(2):
                nc.tensor.transpose(
                    pairs_t[:, (2 * j + u) * P : (2 * j + u + 1) * P], words[:, word + u : word + 2 * P : 2], ident
                )
        banks.append(pairs_t)
    return banks


def group_words(banks, grouped, copies):
    n = grouped.shape[1] // FFN
    grouped_words = grouped.bitcast(F32).rearrange("p (n r u) -> p n r u", n=n, u=2)
    for b, pairs_t in enumerate(banks):
        count = min(2, n - 2 * b)
        copies[b % len(copies)](
            out=grouped_words[:, 2 * b : 2 * b + count],
            in_=pairs_t[:, 0 : count * 2 * P].rearrange("p (j u r) -> p j r u", j=count, u=2),
        )


def tile_tsh_mid_block_pb_t_kernel(tc, h, w_f2, b_f2, res1, g2, be2, w_h, b_h, out):
    nc = tc.nc
    h_rows = h.flatten_outer_dims().rearrange("(p j) k -> p j k", p=P)
    res_rows = res1.flatten_outer_dims().rearrange("(p j) m -> p j m", p=P)
    out_rows = out.flatten_outer_dims().rearrange("(p j) o -> p j o", p=P)

    with ExitStack() as ctx:
        const = ctx.enter_context(tc.tile_pool(name="const", bufs=1))
        loads = ctx.enter_context(tc.tile_pool(name="loads", bufs=4))
        work = ctx.enter_context(tc.tile_pool(name="work", bufs=3))
        ahead = ctx.enter_context(tc.tile_pool(name="ahead", bufs=4))
        bias_bank = ctx.enter_context(tc.psum_pool(name="bias_bank", bufs=1))
        ring = ctx.enter_context(tc.psum_pool(name="ring", bufs=7))

        def new_bank():
            return ring.tile([P, BANK], F32, name="bank", tag="bank")

        ident = const.tile([P, P], F32)
        make_identity(nc, ident[:])
        ident_bf16 = const.tile([P, P], BF16)
        eps = const.tile([P, 1], F32)
        nc.vector.memset(eps[:], LN_EPS)
        bias_rows = const.tile([P, MID + D_OUT], BF16)
        nc.vector.memset(bias_rows[:], 0.0)
        ones = const.tile([P, P], BF16)
        nc.vector.memset(ones[:], 1.0)
        vec_rows = const.tile([P, MID], BF16)
        nc.vector.memset(vec_rows[:], 0.0)
        nc.vector.tensor_copy(out=ident_bf16[:], in_=ident[:])
        table_warm = const.tile([P, 1], F32)
        nc.scalar.activation(out=table_warm[:], in_=eps[:], func=ACT.Abs_reciprocal_sqrt)

        w1_sb = const.tile([P, PACK, FFN], BF16)
        w1_grouped = const.tile([P, PACK * FFN], BF16, align_bytes=64)
        w1_codes = const.tile([P, MID], U32, align_bytes=64)
        w1_scales = const.tile([P, MID], U8, align_bytes=64)
        b1_all = bias_bank.tile([P, MID], F32)
        b2_all = const.tile([P, D_OUT], F32)
        vec_rows_f32 = const.tile([P, MID], F32)
        vec_cols = const.tile([P, PACK, 2], F32)
        gain = [vec_cols[:, t, 0:1] for t in range(PACK)]
        shift = [vec_cols[:, t, 1:2] for t in range(PACK)]
        w2_sb = const.tile([P, D_OUT // P, MID], BF16)
        w2_grouped = const.tile([P, D_OUT // P * MID], BF16, align_bytes=64)
        w2_codes = const.tile([P, D_OUT], U32, align_bytes=64)
        w2_scales = const.tile([P, D_OUT], U8, align_bytes=64)

        def load_first_weights():
            w_rows = w_f2.rearrange("(m t) k -> m t k", t=PACK)
            for half in (slice(0, 2), slice(2, 4)):
                nc.sync.dma_start(out=w1_sb[:, half, :], in_=w_rows[:, half, :])
            nc.scalar.dma_start(out=bias_rows[0:1, 0:MID], in_=b_f2.rearrange("(o m) -> o m", o=1))
            nc.scalar.dma_start(out=bias_rows[0:1, MID : MID + D_OUT], in_=b_h.rearrange("(o m) -> o m", o=1))

        def load_last_weights():
            nc.sync.dma_start(out=vec_rows[0:1, :], in_=g2.rearrange("(o m) -> o m", o=1))
            nc.sync.dma_start(out=vec_rows[1:2, :], in_=be2.rearrange("(o m) -> o m", o=1))
            nc.sync.dma_start(out=w2_sb[:], in_=w_h.rearrange("(r p) m -> p r m", p=P))

        def prepare_first_weights():
            banks = transpose_words(nc, new_bank, w1_sb[:], ident[:])
            group_words(banks, w1_grouped[:], [nc.scalar.copy, nc.vector.tensor_copy])
            nc.vector.quantize_mx(out=w1_codes[:].bitcast(FP8X4), scales=w1_scales[:], in_=w1_grouped[:])

        def spread_first_bias():
            for t in range(PACK):
                nc.tensor.matmul(
                    out=b1_all[:, t * P : (t + 1) * P], lhsT=ones[:], rhs=bias_rows[:, t:MID:PACK], start=True, stop=True
                )

        def prepare_last_weights():
            b2_spread = new_bank()
            nc.tensor.matmul(
                out=b2_spread[:, 0:D_OUT], lhsT=ones[:], rhs=bias_rows[:, MID : MID + D_OUT], start=True, stop=True
            )
            nc.scalar.copy(out=b2_all[:], in_=b2_spread[:, 0:D_OUT])
            nc.gpsimd.tensor_scalar(
                out=vec_rows_f32[:], in0=vec_rows[:], scalar1=1.0, scalar2=0.0, op0=MULT, op1=ADD
            )
            vec_t = new_bank()
            for t in range(PACK):
                nc.tensor.transpose(vec_t[:, t * P : (t + 1) * P], vec_rows_f32[:, t:MID:PACK], ident[:])
            nc.scalar.copy(out=vec_cols[:], in_=vec_t[:].rearrange("p (t v) -> p t v", t=PACK)[:, :, 0:2])
            group_words(transpose_words(nc, new_bank, w2_sb[:], ident[:]), w2_grouped[:], [nc.scalar.copy])

        def quantise_last_weight():
            nc.vector.quantize_mx(out=w2_codes[:].bitcast(FP8X4), scales=w2_scales[:], in_=w2_grouped[:])

        h_in, res_in, h_pairs, grouped_of, h_packed = {}, {}, {}, {}, {}
        ffn_of, biased_of, res_biased, res2_of, sums_of, square_sums_of = {}, {}, {}, {}, {}, {}
        neg_mean_of, rstd_of, normed_of, chunks_of, n_planes, n_grouped, n_packed = {}, {}, {}, {}, {}, {}, {}

        def load(g):
            n, first = SIZES[g], STARTS[g]
            h_sb = loads.tile([P, n, FFN], BF16)
            nc.sync.dma_start(out=h_sb[:], in_=h_rows[:, first : first + n, :])
            res_sb = loads.tile([P, n, MID], BF16)
            nc.sync.dma_start(out=res_sb[:], in_=res_rows[:, first : first + n, :])
            h_in[g], res_in[g] = h_sb, res_sb

        def transpose_h(g):
            h_pairs[g] = transpose_words(nc, new_bank, h_in[g][:], ident[:])

        def mate(g):
            return g >= 4 and g < GROUPS and SIZES[g] == SIZES[g - 4]

        def group_h(g):
            width = SIZES[g] * FFN
            grouped = work.tile([P, 2 * width if mate(g) else width], BF16, align_bytes=64)
            group_words(h_pairs[g], grouped[:, 0:width], [nc.scalar.copy])
            grouped_of[g] = grouped
            if mate(g):
                n_grouped[g - 4] = grouped[:, width : 2 * width]

        def on_tensor(g, j):
            return j > 0 and j == SIZES[g] - 1

        def add_bias_on_tensor(g):
            res_biased[g] = ahead.tile([P, SIZES[g], MID], F32, name="res_b")
            for j in range(SIZES[g]):
                if on_tensor(g, j):
                    biased = new_bank()
                    nc.tensor.matmul(out=biased[:], lhsT=ident_bf16[:], rhs=res_in[g][:, j, :], start=True, stop=False)
                    nc.tensor.matmul(out=biased[:], lhsT=ones[:], rhs=bias_rows[:, 0:MID], start=False, stop=True)
                    biased_of[g] = biased

        def copy_biased(g):
            for j in range(SIZES[g]):
                if on_tensor(g, j):
                    nc.scalar.copy(
                        out=res_biased[g][:, j, :].rearrange("p (t m) -> p t m", t=PACK),
                        in_=biased_of[g][:].rearrange("p (m t) -> p t m", t=PACK),
                    )

        def add_bias(g):
            n = sum(not on_tensor(g, j) for j in range(SIZES[g]))
            nc.vector.tensor_tensor(
                out=res_biased[g][:, 0:n, :].rearrange("p j (t m) -> p j t m", t=PACK),
                in0=res_in[g][:, 0:n, :].rearrange("p j (m t) -> p j t m", t=PACK),
                in1=b1_all[:].rearrange("p (t m) -> p t m", t=PACK).unsqueeze(1).to_broadcast([P, n, PACK, P]),
                op=ADD,
            )

        def quantise_h(g):
            width = SIZES[g] * P
            columns = 2 * width if mate(g) else width
            codes = work.tile([P, columns], U32, align_bytes=64)
            scales = work.tile([P, columns], U8, align_bytes=64)
            nc.vector.quantize_mx(out=codes[:].bitcast(FP8X4), scales=scales[:], in_=grouped_of[g][:])
            h_packed[g] = (codes[:, 0:width], scales[:, 0:width])
            if mate(g):
                n_packed[g - 4] = (codes[:, width : 2 * width], scales[:, width : 2 * width])

        def first_matmul(g):
            h_codes, h_scales = h_packed[g]
            ffn_of[g] = []
            for j in range(SIZES[g]):
                tokens = slice(j * P, (j + 1) * P)
                ffn = new_bank()
                nc.tensor.matmul_mx(
                    out=ffn[:],
                    lhsT=h_codes[:, tokens].bitcast(FP8X4),
                    lhsT_scale=h_scales[:, tokens],
                    rhs=w1_codes[:].bitcast(FP8X4),
                    rhs_scale=w1_scales[:],
                    start=True,
                    stop=True,
                )
                ffn_of[g].append(ffn)

        def add_residual(g):
            n = SIZES[g]
            res2_of[g] = work.tile([P, n, MID], F32, name="res2")
            sums_of[g] = work.tile([P, n], F32, name="sums")
            for j in range(n):
                nc.vector.scalar_tensor_tensor(
                    out=res2_of[g][:, j, :], in0=ffn_of[g][j][:], scalar=1.0, in1=res_biased[g][:, j, :],
                    op0=MULT, op1=ADD, accum_out=sums_of[g][:, j : j + 1],
                )

        def squares(g):
            n = SIZES[g]
            ignored = work.tile([P, n, MID], BF16)
            square_sums = work.tile([P, n], F32)
            for j in range(n):
                nc.scalar.activation(
                    out=ignored[:, j, :], in_=res2_of[g][:, j, :], func=ACT.Square,
                    bias=sums_of[g][:, j : j + 1], scale=-float(MID), accum_out=square_sums[:, j : j + 1],
                )
            square_sums_of[g] = square_sums

        def negative_mean(g):
            neg_mean = work.tile([P, SIZES[g]], F32)
            nc.scalar.mul(out=neg_mean[:], in_=sums_of[g][:], mul=-1.0 / MID)
            neg_mean_of[g] = neg_mean

        def reciprocal_deviation(g):
            rstd = work.tile([P, SIZES[g]], F32)
            nc.scalar.activation(
                out=rstd[:], in_=square_sums_of[g][:], func=ACT.Abs_reciprocal_sqrt, scale=1.0 / MID**3, bias=eps[:, 0:1]
            )
            rstd_of[g] = rstd

        def last(g):
            return g >= GROUPS - VECTOR_GROUPS

        def normalise(g):
            normed = work.tile([P, SIZES[g], MID], F32)
            for j in range(SIZES[g]):
                engine = nc.vector if (j == 3 and g % 2 == 0) or last(g) else nc.gpsimd
                engine.tensor_scalar(
                    out=normed[:, j, :], in0=res2_of[g][:, j, :], scalar1=neg_mean_of[g][:, j : j + 1],
                    scalar2=rstd_of[g][:, j : j + 1], op0=ADD, op1=MULT,
                )
            normed_of[g] = normed

        def transpose_norm(g):
            n = SIZES[g]
            chunks_of[g] = []
            for t in range(PACK):
                if t % (PACK // n) == 0:
                    chunks = new_bank()
                first = t % (PACK // n) * n
                for j in range(n):
                    nc.tensor.transpose(
                        chunks[:, (first + j) * P : (first + j + 1) * P], normed_of[g][:, j, t * P : (t + 1) * P], ident[:]
                    )
                chunks_of[g].append(chunks[:, first * P : (first + n) * P])
            n_planes[g] = work.tile([P, PACK, n * P], BF16, name="planes")

        def scale_and_shift(g, ts):
            for t in ts:
                nc.scalar.activation(
                    out=n_planes[g][:, t, :], in_=chunks_of[g][t], func=ACT.Identity, scale=gain[t], bias=shift[t]
                )

        def group_norm(g):
            if not mate(g + 4):
                own = work.tile([P, SIZES[g] * P * PACK], BF16, align_bytes=64)
                n_grouped[g] = own[:]
            engine = nc.vector if last(g) else nc.gpsimd
            engine.tensor_scalar(
                out=n_grouped[g].rearrange("p (w i t) -> p w t i", i=RUN, t=PACK),
                in0=n_planes[g][:].rearrange("p t (w i) -> p w t i", i=RUN),
                scalar1=1.0, scalar2=0.0, op0=MULT, op1=ADD,
            )

        def quantise_norm(g):
            if not mate(g + 4):
                n_codes = work.tile([P, SIZES[g] * P], U32, align_bytes=64)
                n_scales = work.tile([P, SIZES[g] * P], U8, align_bytes=64)
                nc.vector.quantize_mx(out=n_codes[:].bitcast(FP8X4), scales=n_scales[:], in_=n_grouped[g])
                n_packed[g] = (n_codes[:], n_scales[:])

        def second_matmul(g):
            n, first = SIZES[g], STARTS[g]
            n_codes, n_scales = n_packed[g]
            result = work.tile([P, n, D_OUT], F32)
            for b in range(0, n, 2):
                count = min(2, n - b)
                head = new_bank()
                for j in range(count):
                    tokens = slice((b + j) * P, (b + j + 1) * P)
                    nc.tensor.matmul_mx(
                        out=head[:, j * D_OUT : (j + 1) * D_OUT],
                        lhsT=n_codes[:, tokens].bitcast(FP8X4),
                        lhsT_scale=n_scales[:, tokens],
                        rhs=w2_codes[:].bitcast(FP8X4),
                        rhs_scale=w2_scales[:],
                        start=True,
                        stop=True,
                    )
                nc.vector.tensor_tensor(
                    out=result[:, b : b + count, :],
                    in0=head[:, 0 : count * D_OUT].rearrange("p (j o) -> p j o", j=count),
                    in1=b2_all[:].unsqueeze(1).to_broadcast([P, count, D_OUT]),
                    op=ADD,
                )
            nc.sync.dma_start(out=out_rows[:, first : first + n, :], in_=result[:])

        def live(g):
            return 0 <= g < GROUPS

        with tc.manual_schedule():
            load_first_weights()
            for k in range(GROUPS + 7):
                if live(k):
                    load(k)
                if k == 1:
                    load_last_weights()
                if live(k - 5):
                    squares(k - 5)
                    negative_mean(k - 5)
                if k == 2:
                    prepare_first_weights()
                if live(k - 2):
                    transpose_h(k - 2)
                if k == 2:
                    spread_first_bias()
                if live(k - 4) and last(k - 4):
                    first_matmul(k - 4)
                if live(k - 6):
                    transpose_norm(k - 6)
                    scale_and_shift(k - 6, [0])
                if live(k - 5):
                    reciprocal_deviation(k - 5)
                if live(k - 6):
                    scale_and_shift(k - 6, [1])
                if live(k - 6):
                    scale_and_shift(k - 6, [2, 3])
                if live(k - 2):
                    group_h(k - 2)
                if k == 3:
                    prepare_last_weights()
                if live(k - 2):
                    add_bias_on_tensor(k - 2)
                    add_bias(k - 2)
                if live(k - 4) and not last(k - 4):
                    first_matmul(k - 4)
                if live(k - 3):
                    quantise_h(k - 3)
                if live(k - 4) and last(k - 4):
                    add_residual(k - 4)
                if live(k - 7):
                    quantise_norm(k - 7)
                if live(k - 5) and not last(k - 5):
                    normalise(k - 5)
                if live(k - 2):
                    copy_biased(k - 2)
                if live(k - 4) and not last(k - 4):
                    add_residual(k - 4)
                if live(k - 5) and last(k - 5):
                    normalise(k - 5)
                if k == 5:
                    quantise_last_weight()
                if live(k - 6):
                    group_norm(k - 6)
                if live(k - 7):
                    second_matmul(k - 7)
